import numpy as np
import ml_dtypes


def mxq(x, axis, fmt="e4m3"):
    dtype, down = {"e4m3": (ml_dtypes.float8_e4m3fn, 7), "e5m2": (ml_dtypes.float8_e5m2, 14)}[fmt]
    v = np.moveaxis(np.asarray(x, np.float32).astype(ml_dtypes.bfloat16).astype(np.float64), axis, -1)
    blocks = v.reshape(v.shape[:-1] + (-1, 32))
    amax = np.abs(blocks).max(-1, keepdims=True)
    byte = np.maximum(np.where(amax > 0, np.frexp(amax)[1] - 1 + 127, 0) - down, 1)
    scale = np.exp2(byte - 127.0)
    codes = (blocks / scale).astype(np.float32).astype(dtype).astype(np.float64)
    return np.moveaxis((codes * scale).reshape(v.shape), -1, axis)


WIDE = False


def mx_kscale(k):
    if not WIDE:
        return np.ones(k)
    levels = np.array([10, -10, 5, -5, 0])
    a = np.random.permutation(np.resize(levels, k // 512 * 4)).reshape(k // 512, 4)
    idx = np.arange(k)
    return np.exp2(a[idx // 512, idx % 128 // 32])


BF16 = ml_dtypes.bfloat16


def bf(x):
    return np.asarray(x, np.float32).astype(BF16)


def f64(x):
    return np.asarray(x).astype(np.float64)


B, C, LL, LM, LS = 256, 1024, 2, 4, 6
SOFTMAX_SCALE = 10.0


def softmax(v, axis):
    e = np.exp(v - v.max(axis=axis, keepdims=True))
    return e / e.sum(axis=axis, keepdims=True)


def setup_inputs():
    s = mx_kscale(2 * C)[:C][None, :, None]
    g = lambda l: np.random.standard_normal((B, C, l))
    return {"left": bf(g(LL) * 0.3 / np.sqrt(2 * C) / s), "right": bf(g(LL) * 0.3 / np.sqrt(2 * C) / s), "mid": bf(g(LM) * s),
            "sc00": bf(g(LS) * 0.1), "sc01": bf(g(LS) * 0.1), "sc10": bf(g(LS) * 0.1), "sc11": bf(g(LS) * 0.1)}


def reference(left, right, mid, sc00, sc01, sc10, sc11):
    left, right, mid, sc00, sc01, sc10, sc11 = (f64(a) for a in (left, right, mid, sc00, sc01, sc10, sc11))
    b, c, lm = mid.shape
    left_cat = np.concatenate([left, right], axis=2)
    raw_l = [np.concatenate([sc00, sc10], axis=2), sc10]
    lcat = left_cat.shape[2]
    n = min(-(-lm // 2), -(-lcat // 2), b)
    X = mid[:, :, : 2 * n].reshape(b, c, n, 2).transpose(2, 0, 1, 3)
    X = np.pad(X, ((0, 0), (0, 0), (0, 0), (1, 0)))
    W = left_cat[:, :, : 2 * n].reshape(b, c, n, 2).transpose(2, 0, 1, 3)
    win = np.stack([X[..., 0:2], X[..., 1:3]], axis=3)
    A = win.transpose(0, 1, 3, 4, 2).reshape(n, b * 2, 2 * c)
    Wm = W.transpose(0, 3, 2, 1).reshape(n, 2 * c, b)
    scores = (mxq(A, 2, "e4m3") @ mxq(Wm, 1, "e4m3")) * SOFTMAX_SCALE
    scores = scores.reshape(n, b, 2, b).transpose(0, 1, 3, 2)
    att = softmax(scores, 2)
    att = np.pad(att, ((0, 0), (0, 0), (0, c - b), (0, 0)))
    ls = sc10.shape[2]
    outs = []
    for rl in raw_l:
        centers = np.moveaxis(rl[:, :, :n], 2, 0)[..., None]
        y = np.concatenate([att, centers], axis=3)
        y = np.moveaxis(y, 0, 2).reshape(b, c, 3 * n)
        pad = ls - y.shape[2]
        if pad > 0:
            y = np.pad(y, ((0, 0), (0, 0), (0, pad)))
        outs.append(y)
    return tuple(outs)

@@ -1,0 +1,211 @@
+from contextlib import ExitStack
+
+import concourse.mybir as mybir
+from concourse.masks import make_identity
+
+F32 = mybir.dt.float32
+BF16 = mybir.dt.bfloat16
+U32 = mybir.dt.uint32
+U8 = mybir.dt.uint8
+FP8X4 = mybir.dt.float8_e4m3fn_x4
+ALU = mybir.AluOpType
+ACT = mybir.ActivationFunctionType
+
+P = 128
+B = 256
+C = 1024
+H = B // P
+NA = 256
+COLS = 6
+SCALE = 10.0
+
+FLOPS = 2 * 2 * 512 * 256 * 2048
+BYTES = 2 * (B * C * 2 * 2) + B * C * 4 * 2 + 2 * (B * C * 2 * 2) + 2 * (B * C * COLS * 4)
+
+VECTOR_BANKS = (2, 5, 8, 11, 14)
+
+
+def tile_contextualattention_kernel(tc, left, right, mid, sc00, sc01, sc10, sc11, out_0, out_1):
+    nc = tc.nc
+    outs = (out_0, out_1)
+    scs = (sc00, sc10)
+    with ExitStack() as ctx:
+        keep = ctx.enter_context(tc.tile_pool(name="keep", bufs=1))
+        stage = ctx.enter_context(tc.tile_pool(name="stage", bufs=3))
+        psum_t = ctx.enter_context(tc.psum_pool(name="psum_t", bufs=4))
+        psum_s = ctx.enter_context(tc.psum_pool(name="psum_s", bufs=4))
+
+        mid_sb = [keep.tile([P, C * 4], BF16, name="mid%d" % h) for h in range(H)]
+        lc_sb = [[keep.tile([P, C * 2], BF16, name="lc%d%d" % (i, h)) for h in range(H)] for i in range(2)]
+        sc_sb = [[keep.tile([P, C * COLS], BF16, name="sc%d%d" % (h, r)) for r in range(2)] for h in range(H)]
+
+        def rows(ap, h):
+            return ap[h * P : (h + 1) * P].rearrange("b c j -> b (c j)")
+
+        nc.sync.dma_start(out=mid_sb[0][:], in_=rows(mid, 0))
+        nc.sync.dma_start(out=lc_sb[0][0][:], in_=rows(left, 0))
+        nc.sync.dma_start(out=lc_sb[0][1][:], in_=rows(left, 1))
+        nc.sync.dma_start(out=mid_sb[1][:], in_=rows(mid, 1))
+        nc.sync.dma_start(out=lc_sb[1][0][:], in_=rows(right, 0))
+        nc.sync.dma_start(out=lc_sb[1][1][:], in_=rows(right, 1))
+        for h in range(H):
+            for r in range(2):
+                nc.sync.dma_start(out=sc_sb[h][r][:], in_=rows(scs[r], h))
+
+        ident = keep.tile([P, P], F32, name="ident")
+        make_identity(nc, ident[:])
+        warm = keep.tile([P, 1], F32, name="warm")
+        warm2 = keep.tile([P, 1], F32, name="warm2")
+        nc.vector.memset(warm[:], 0.0)
+        nc.scalar.activation(out=warm2[:], in_=warm[:], func=ACT.Exp)
+
+        o_sb = [[keep.tile([P, C * COLS], F32, name="o%d%d" % (h, r)) for r in range(2)] for h in range(H)]
+        for r in range(2):
+            nc.vector.memset(o_sb[0][r][:, NA * COLS :], 0.0)
+            nc.gpsimd.memset(o_sb[1][r][:, NA * COLS :], 0.0)
+
+        m_codes = keep.tile([P, 2048], U32, name="m_codes", align_bytes=64)
+        m_scales = keep.tile([P, 2048], U8, name="m_scales", align_bytes=64)
+        l_codes = keep.tile([P, 2048], U32, name="l_codes", align_bytes=64)
+        l_scales = keep.tile([P, 2048], U8, name="l_scales", align_bytes=64)
+
+        counter = [0]
+
+        def copy_out(dst, bank):
+            src = bank[:].bitcast(BF16).rearrange("p (t w e) -> p e w t", t=4, w=P, e=2)
+            if counter[0] in VECTOR_BANKS:
+                nc.vector.tensor_copy(out=dst, in_=src)
+            else:
+                nc.scalar.copy(out=dst, in_=src)
+            counter[0] += 1
+
+        def quantise(grouped, codes, scales, unit):
+            cols = slice(unit * 512, (unit + 1) * 512)
+            nc.vector.quantize_mx(
+                out=codes[:, cols].bitcast(FP8X4),
+                scales=scales[:, cols],
+                in_=grouped[:].rearrange("p a b w t -> p (a b w t)"),
+            )
+
+        def prepare_mid(h, i):
+            words = mid_sb[h][:].bitcast(F32).rearrange("b (c i) -> b c i", i=2)
+            grouped = stage.tile([P, 2, 2, P, 4], BF16, tag="grouped", name="grouped_m", align_bytes=64)
+            for g in range(2):
+                bank = psum_t.tile([P, 512], F32, tag="xt", name="xt_m")
+                for t in range(4):
+                    c0 = 512 * g + P * t
+                    nc.tensor.transpose(bank[:, t * P : (t + 1) * P], words[:, c0 : c0 + P, i], ident[:])
+                copy_out(grouped[:, g], bank)
+            quantise(grouped, m_codes, m_scales, 2 * h + i)
+
+        def prepare_lc(i, g):
+            grouped = stage.tile([P, 2, 2, P, 4], BF16, tag="grouped", name="grouped_l", align_bytes=64)
+            for ho in range(H):
+                words = lc_sb[i][ho][:].bitcast(F32)
+                bank = psum_t.tile([P, 512], F32, tag="xt", name="xt_l")
+                for t in range(4):
+                    c0 = 512 * g + P * t
+                    nc.tensor.transpose(bank[:, t * P : (t + 1) * P], words[:, c0 : c0 + P], ident[:])
+                copy_out(grouped[:, :, ho], bank)
+            quantise(grouped, l_codes, l_scales, 2 * i + g)
+
+        e_sb = [keep.tile([P, 2, 2, NA], F32, name="e%d" % h) for h in range(H)]
+        mx = keep.tile([P, 8], F32, name="mx")
+        nb = keep.tile([P, 8], F32, name="nb")
+        sm = keep.tile([P, 8], F32, name="sm")
+        rs = keep.tile([P, 8], F32, name="rs")
+
+        def m_op(h, i, g, e):
+            lo = (((h * 2 + i) * 2 + g) * 2 + e) * P
+            return slice(lo, lo + P)
+
+        def l_op(i, g, e):
+            lo = ((i * 2 + g) * 2 + e) * 2 * P
+            return slice(lo, lo + 2 * P)
+
+        def scores(h, i):
+            acc = psum_s.tile([P, 2 * NA], F32, tag="acc", name="acc")
+            plans = (
+                [(g, 0, 1) for g in range(2)],
+                [(g, e, e) for g in range(2) for e in range(2)],
+            )
+            for t in range(2):
+                plan = plans[t]
+                for n, (g, em, el) in enumerate(plan):
+                    nc.tensor.matmul_mx(
+                        out=acc[:, t * NA : (t + 1) * NA],
+                        lhsT=m_codes[:, m_op(h, i, g, em)].bitcast(FP8X4),
+                        lhsT_scale=m_scales[:, m_op(h, i, g, em)],
+                        rhs=l_codes[:, l_op(i, g, el)].bitcast(FP8X4),
+                        rhs_scale=l_scales[:, l_op(i, g, el)],
+                        start=(n == 0),
+                        stop=(n == len(plan) - 1),
+                    )
+            k = (h * 2 + i) * 2
+            nc.vector.tensor_reduce(
+                out=mx[:, k : k + 2],
+                in_=acc[:].rearrange("p (t o) -> p t o", t=2),
+                axis=mybir.AxisListType.X,
+                op=ALU.max,
+            )
+            nc.vector.tensor_scalar(out=nb[:, k : k + 2], in0=mx[:, k : k + 2], scalar1=-SCALE, scalar2=None, op0=ALU.mult)
+            for t in range(2):
+                nc.scalar.activation(
+                    out=e_sb[h][:, i, t, :],
+                    in_=acc[:, t * NA : (t + 1) * NA],
+                    func=ACT.Exp,
+                    bias=nb[:, k + t : k + t + 1],
+                    scale=SCALE,
+                    accum_out=sm[:, k + t : k + t + 1],
+                )
+            nc.vector.reciprocal(out=rs[:, k : k + 2], in_=sm[:, k : k + 2])
+            for t in range(2):
+                nc.vector.tensor_scalar(
+                    out=e_sb[h][:, i, t, :],
+                    in0=e_sb[h][:, i, t, :],
+                    scalar1=rs[:, k + t : k + t + 1],
+                    scalar2=None,
+                    op0=ALU.mult,
+                )
+
+        def shortcut(engine_copy, h, r, lo, hi):
+            dst = o_sb[h][r][:, lo * COLS : hi * COLS].rearrange("p (c i t) -> p c i t", i=2, t=3)[:, :, :, 2]
+            src = sc_sb[h][r][:, lo * COLS : hi * COLS].rearrange("p (c j) -> p c j", j=COLS)[:, :, 0:2]
+            engine_copy(out=dst, in_=src)
+
+        def attention(h, r):
+            dst = o_sb[h][r][:, : NA * COLS].rearrange("p (o i t) -> p o i t", i=2, t=3)[:, :, :, 0:2]
+            nc.vector.tensor_copy(out=dst, in_=e_sb[h][:].rearrange("p i t o -> p o i t"))
+
+        def store(h, r, lo, hi):
+            nc.sync.dma_start(
+                out=outs[r][h * P : (h + 1) * P, lo:hi, :].rearrange("b c j -> b (c j)"),
+                in_=o_sb[h][r][:, lo * COLS : hi * COLS],
+            )
+
+        prepare_mid(0, 0)
+        prepare_mid(0, 1)
+        prepare_lc(0, 0)
+        prepare_lc(0, 1)
+        scores(0, 0)
+        prepare_mid(1, 0)
+        prepare_mid(1, 1)
+        scores(1, 0)
+        prepare_lc(1, 0)
+        prepare_lc(1, 1)
+        scores(0, 1)
+        scores(1, 1)
+
+        for r in range(2):
+            shortcut(nc.vector.tensor_copy, 0, r, 0, C)
+            store(0, r, NA, C)
+        for r in range(2):
+            attention(0, r)
+            store(0, r, 0, NA)
+        for r in range(2):
+            shortcut(nc.scalar.copy, 1, r, NA, C)
+            store(1, r, NA, C)
+        for r in range(2):
+            shortcut(nc.vector.tensor_copy, 1, r, 0, NA)
+            attention(1, r)
+            store(1, r, 0, NA)

@@ -18,11 +18,15 @@ H = B // P
 NA = 256
 COLS = 6
 SCALE = 10.0
+ROW = NA * COLS
+SLOT_ROWS = (C - NA) // NA
+SLOTS = 2
+NZ = SLOTS * SLOT_ROWS + 1
 
 FLOPS = 2 * 2 * 512 * 256 * 2048
 BYTES = 2 * (B * C * 2 * 2) + B * C * 4 * 2 + 2 * (B * C * 2 * 2) + 2 * (B * C * COLS * 4)
 
-VECTOR_BANKS = (2, 5, 8, 11, 14)
+COPY_ENGINE = "SSSSVVVSSSSSVVVS"
 
 
 def tile_contextualattention_kernel(tc, left, right, mid, sc00, sc01, sc10, sc11, out_0, out_1):
@@ -35,85 +39,124 @@ def tile_contextualattention_kernel(tc, left, right, mid, sc00, sc01, sc10, sc11
         psum_t = ctx.enter_context(tc.psum_pool(name="psum_t", bufs=4))
         psum_s = ctx.enter_context(tc.psum_pool(name="psum_s", bufs=4))
 
-        mid_sb = [keep.tile([P, C * 4], BF16, name="mid%d" % h) for h in range(H)]
-        lc_sb = [[keep.tile([P, C * 2], BF16, name="lc%d%d" % (i, h)) for h in range(H)] for i in range(2)]
-        sc_sb = [[keep.tile([P, C * COLS], BF16, name="sc%d%d" % (h, r)) for r in range(2)] for h in range(H)]
-
-        def rows(ap, h):
-            return ap[h * P : (h + 1) * P].rearrange("b c j -> b (c j)")
-
-        nc.sync.dma_start(out=mid_sb[0][:], in_=rows(mid, 0))
-        nc.sync.dma_start(out=lc_sb[0][0][:], in_=rows(left, 0))
-        nc.sync.dma_start(out=lc_sb[0][1][:], in_=rows(left, 1))
-        nc.sync.dma_start(out=mid_sb[1][:], in_=rows(mid, 1))
-        nc.sync.dma_start(out=lc_sb[1][0][:], in_=rows(right, 0))
-        nc.sync.dma_start(out=lc_sb[1][1][:], in_=rows(right, 1))
-        for h in range(H):
-            for r in range(2):
-                nc.sync.dma_start(out=sc_sb[h][r][:], in_=rows(scs[r], h))
-
         ident = keep.tile([P, P], F32, name="ident")
         make_identity(nc, ident[:])
+
+        ctx.enter_context(tc.manual_schedule())
+
+        mid_sb = [keep.tile([P, C * 4], BF16, name="mid%d" % h) for h in range(H)]
+        lc_sb = [[keep.tile([P, C * 2], BF16, name="lc%d%d" % (i, h)) for h in range(H)] for i in range(2)]
+        sca = [[keep.tile([P, ROW], BF16, name="sca%d%d" % (h, r)) for r in range(2)] for h in range(H)]
+        scz = keep.tile([P, (NZ + SLOTS * SLOT_ROWS) * ROW], BF16, name="scz")
+        grid = scz[:].rearrange("p (n g) -> p n g", g=ROW)
+        zt = [[keep.tile([P, SLOT_ROWS * ROW], F32, name="zt%d%d" % (h, r)) for r in range(2)] for h in range(H)]
+        at = [[keep.tile([P, ROW], F32, name="at%d%d" % (h, r)) for r in range(2)] for h in range(H)]
+        w_sb = [keep.tile([P, COLS, NA], F32, name="w%d" % h) for h in range(H)]
+
+        def rows(ap, h, lo, hi):
+            return ap[h * P : (h + 1) * P, lo:hi, :].rearrange("b c j -> b (c j)")
+
+        def load_z(h, r):
+            lo = (NZ + r * SLOT_ROWS) * ROW
+            nc.sync.dma_start(out=scz[:, lo : lo + SLOT_ROWS * ROW], in_=rows(scs[r], h, NA, C))
+
+        load_z(0, 0)
+        load_z(0, 1)
+        nc.sync.dma_start(out=mid_sb[0][:], in_=rows(mid, 0, 0, C))
+        nc.sync.dma_start(out=lc_sb[0][0][:], in_=rows(left, 0, 0, C))
+        nc.sync.dma_start(out=lc_sb[0][1][:], in_=rows(left, 1, 0, C))
+        nc.sync.dma_start(out=mid_sb[1][:], in_=rows(mid, 1, 0, C))
+        nc.sync.dma_start(out=lc_sb[1][0][:], in_=rows(right, 0, 0, C))
+        nc.sync.dma_start(out=lc_sb[1][1][:], in_=rows(right, 1, 0, C))
+        for h in range(H):
+            for r in range(2):
+                nc.sync.dma_start(out=sca[h][r][:], in_=rows(scs[r], h, 0, NA))
+
         warm = keep.tile([P, 1], F32, name="warm")
         warm2 = keep.tile([P, 1], F32, name="warm2")
         nc.vector.memset(warm[:], 0.0)
         nc.scalar.activation(out=warm2[:], in_=warm[:], func=ACT.Exp)
+        nc.vector.memset(scz[:, : NZ * ROW].bitcast(F32), 0.0)
 
-        o_sb = [[keep.tile([P, C * COLS], F32, name="o%d%d" % (h, r)) for r in range(2)] for h in range(H)]
+        def expand(copy, h, r, m):
+            q = r * SLOT_ROWS + m
+            n0 = NZ + q
+            k = q + 1
+            src = grid[:, n0 - 2 * k : n0 + 1 : k, :].rearrange("p t (c j) -> p c j t", j=COLS)[:, :, 0:2, :]
+            dst = zt[h][r][:, m * ROW : (m + 1) * ROW].rearrange("p (c i t) -> p c i t", i=2, t=3)
+            copy(out=dst, in_=src)
+
+        def store_z(h, r):
+            nc.sync.dma_start(out=rows(outs[r], h, NA, C), in_=zt[h][r][:])
+
+        def store_a(h, r):
+            nc.sync.dma_start(out=rows(outs[r], h, 0, NA), in_=at[h][r][:])
+
         for r in range(2):
-            nc.vector.memset(o_sb[0][r][:, NA * COLS :], 0.0)
-            nc.gpsimd.memset(o_sb[1][r][:, NA * COLS :], 0.0)
+            for m in range(SLOT_ROWS):
+                expand(nc.vector.tensor_copy, 0, r, m)
+        for r in range(2):
+            load_z(1, r)
+        for r in range(2):
+            store_z(0, r)
 
         m_codes = keep.tile([P, 2048], U32, name="m_codes", align_bytes=64)
         m_scales = keep.tile([P, 2048], U8, name="m_scales", align_bytes=64)
         l_codes = keep.tile([P, 2048], U32, name="l_codes", align_bytes=64)
         l_scales = keep.tile([P, 2048], U8, name="l_scales", align_bytes=64)
 
-        counter = [0]
+        banks = []
+        for first in range(2):
+            for i in range(2):
+                for g in range(2):
+                    banks.append(("m", first, i, g))
+            for g in range(2):
+                for ho in range(2):
+                    banks.append(("l", first, g, ho))
+        bank_tiles = {}
+        grouped_tiles = {}
 
-        def copy_out(dst, bank):
-            src = bank[:].bitcast(BF16).rearrange("p (t w e) -> p e w t", t=4, w=P, e=2)
-            if counter[0] in VECTOR_BANKS:
+        def transposes(n):
+            kind, a, b, c = banks[n]
+            bank = psum_t.tile([P, 512], F32, tag="xt", name="xt")
+            bank_tiles[n] = bank
+            for t in range(4):
+                if kind == "m":
+                    c0 = 512 * c + P * t
+                    src = mid_sb[a][:].bitcast(F32).rearrange("b (c i) -> b c i", i=2)[:, c0 : c0 + P, b]
+                else:
+                    c0 = 512 * b + P * t
+                    src = lc_sb[a][c][:].bitcast(F32)[:, c0 : c0 + P]
+                nc.tensor.transpose(bank[:, t * P : (t + 1) * P], src, ident[:])
+
+        def copy_out(n):
+            kind, a, b, c = banks[n]
+            key = (kind, a, b)
+            if key not in grouped_tiles:
+                grouped_tiles[key] = stage.tile([P, 2, 2, P, 4], BF16, tag="grouped", name="grouped", align_bytes=64)
+            grouped = grouped_tiles[key]
+            dst = grouped[:, c] if kind == "m" else grouped[:, :, c]
+            src = bank_tiles[n][:].bitcast(BF16).rearrange("p (t w e) -> p e w t", t=4, w=P, e=2)
+            if COPY_ENGINE[n] == "V":
                 nc.vector.tensor_copy(out=dst, in_=src)
             else:
                 nc.scalar.copy(out=dst, in_=src)
-            counter[0] += 1
 
-        def quantise(grouped, codes, scales, unit):
+        def quantise(kind, a, b):
+            codes, scales = (m_codes, m_scales) if kind == "m" else (l_codes, l_scales)
+            unit = 2 * a + b
             cols = slice(unit * 512, (unit + 1) * 512)
             nc.vector.quantize_mx(
                 out=codes[:, cols].bitcast(FP8X4),
                 scales=scales[:, cols],
-                in_=grouped[:].rearrange("p a b w t -> p (a b w t)"),
+                in_=grouped_tiles[(kind, a, b)][:].rearrange("p a b w t -> p (a b w t)"),
             )
 
-        def prepare_mid(h, i):
-            words = mid_sb[h][:].bitcast(F32).rearrange("b (c i) -> b c i", i=2)
-            grouped = stage.tile([P, 2, 2, P, 4], BF16, tag="grouped", name="grouped_m", align_bytes=64)
-            for g in range(2):
-                bank = psum_t.tile([P, 512], F32, tag="xt", name="xt_m")
-                for t in range(4):
-                    c0 = 512 * g + P * t
-                    nc.tensor.transpose(bank[:, t * P : (t + 1) * P], words[:, c0 : c0 + P, i], ident[:])
-                copy_out(grouped[:, g], bank)
-            quantise(grouped, m_codes, m_scales, 2 * h + i)
-
-        def prepare_lc(i, g):
-            grouped = stage.tile([P, 2, 2, P, 4], BF16, tag="grouped", name="grouped_l", align_bytes=64)
-            for ho in range(H):
-                words = lc_sb[i][ho][:].bitcast(F32)
-                bank = psum_t.tile([P, 512], F32, tag="xt", name="xt_l")
-                for t in range(4):
-                    c0 = 512 * g + P * t
-                    nc.tensor.transpose(bank[:, t * P : (t + 1) * P], words[:, c0 : c0 + P], ident[:])
-                copy_out(grouped[:, :, ho], bank)
-            quantise(grouped, l_codes, l_scales, 2 * i + g)
-
-        e_sb = [keep.tile([P, 2, 2, NA], F32, name="e%d" % h) for h in range(H)]
         mx = keep.tile([P, 8], F32, name="mx")
         nb = keep.tile([P, 8], F32, name="nb")
         sm = keep.tile([P, 8], F32, name="sm")
         rs = keep.tile([P, 8], F32, name="rs")
+        acc_tiles = {}
 
         def m_op(h, i, g, e):
             lo = (((h * 2 + i) * 2 + g) * 2 + e) * P
@@ -125,6 +168,7 @@ def tile_contextualattention_kernel(tc, left, right, mid, sc00, sc01, sc10, sc11
 
         def scores(h, i):
             acc = psum_s.tile([P, 2 * NA], F32, tag="acc", name="acc")
+            acc_tiles[(h, i)] = acc
             plans = (
                 [(g, 0, 1) for g in range(2)],
                 [(g, e, e) for g in range(2) for e in range(2)],
@@ -141,71 +185,112 @@ def tile_contextualattention_kernel(tc, left, right, mid, sc00, sc01, sc10, sc11
                         start=(n == 0),
                         stop=(n == len(plan) - 1),
                     )
+
+        def row_max(h, i):
             k = (h * 2 + i) * 2
             nc.vector.tensor_reduce(
                 out=mx[:, k : k + 2],
-                in_=acc[:].rearrange("p (t o) -> p t o", t=2),
+                in_=acc_tiles[(h, i)][:].rearrange("p (t o) -> p t o", t=2),
                 axis=mybir.AxisListType.X,
                 op=ALU.max,
             )
             nc.vector.tensor_scalar(out=nb[:, k : k + 2], in0=mx[:, k : k + 2], scalar1=-SCALE, scalar2=None, op0=ALU.mult)
+
+        def exps(h, i):
+            k = (h * 2 + i) * 2
             for t in range(2):
                 nc.scalar.activation(
-                    out=e_sb[h][:, i, t, :],
-                    in_=acc[:, t * NA : (t + 1) * NA],
+                    out=w_sb[h][:, 3 * i + t, :],
+                    in_=acc_tiles[(h, i)][:, t * NA : (t + 1) * NA],
                     func=ACT.Exp,
                     bias=nb[:, k + t : k + t + 1],
                     scale=SCALE,
                     accum_out=sm[:, k + t : k + t + 1],
                 )
-            nc.vector.reciprocal(out=rs[:, k : k + 2], in_=sm[:, k : k + 2])
-            for t in range(2):
-                nc.vector.tensor_scalar(
-                    out=e_sb[h][:, i, t, :],
-                    in0=e_sb[h][:, i, t, :],
-                    scalar1=rs[:, k + t : k + t + 1],
-                    scalar2=None,
-                    op0=ALU.mult,
-                )
 
-        def shortcut(engine_copy, h, r, lo, hi):
-            dst = o_sb[h][r][:, lo * COLS : hi * COLS].rearrange("p (c i t) -> p c i t", i=2, t=3)[:, :, :, 2]
-            src = sc_sb[h][r][:, lo * COLS : hi * COLS].rearrange("p (c j) -> p c j", j=COLS)[:, :, 0:2]
-            engine_copy(out=dst, in_=src)
+        def normalise(h):
+            nc.vector.reciprocal(out=rs[:, 4 * h : 4 * h + 4], in_=sm[:, 4 * h : 4 * h + 4])
+            for i in range(2):
+                for t in range(2):
+                    k = (h * 2 + i) * 2 + t
+                    nc.vector.tensor_scalar(
+                        out=w_sb[h][:, 3 * i + t, :],
+                        in0=w_sb[h][:, 3 * i + t, :],
+                        scalar1=rs[:, k : k + 1],
+                        scalar2=None,
+                        op0=ALU.mult,
+                    )
 
-        def attention(h, r):
-            dst = o_sb[h][r][:, : NA * COLS].rearrange("p (o i t) -> p o i t", i=2, t=3)[:, :, :, 0:2]
-            nc.vector.tensor_copy(out=dst, in_=e_sb[h][:].rearrange("p i t o -> p o i t"))
-
-        def store(h, r, lo, hi):
-            nc.sync.dma_start(
-                out=outs[r][h * P : (h + 1) * P, lo:hi, :].rearrange("b c j -> b (c j)"),
-                in_=o_sb[h][r][:, lo * COLS : hi * COLS],
+        def region_a(h, r):
+            nc.vector.tensor_copy(
+                out=w_sb[h][:].rearrange("p (i t) o -> p i t o", t=3)[:, :, 2, :],
+                in_=sca[h][r][:].rearrange("p (o j) -> p j o", j=COLS)[:, 0:2, :],
             )
+            nc.vector.tensor_copy(
+                out=at[h][r][:].rearrange("p (o j) -> p o j", j=COLS),
+                in_=w_sb[h][:].rearrange("p j o -> p o j"),
+            )
+            store_a(h, r)
 
-        prepare_mid(0, 0)
-        prepare_mid(0, 1)
-        prepare_lc(0, 0)
-        prepare_lc(0, 1)
+        for n in (0, 1, 2, 3):
+            transposes(n)
+        copy_out(0)
+        copy_out(1)
+        transposes(4)
+        transposes(5)
+        copy_out(2)
+        copy_out(3)
+        transposes(6)
+        transposes(7)
+        copy_out(4)
+        copy_out(5)
+        transposes(8)
+        transposes(9)
+        quantise("m", 0, 0)
+        quantise("m", 0, 1)
+        copy_out(6)
+        copy_out(7)
+        transposes(10)
+        transposes(11)
+        quantise("l", 0, 0)
+        copy_out(8)
+        copy_out(9)
+        transposes(12)
+        transposes(13)
+        quantise("l", 0, 1)
+        copy_out(10)
+        copy_out(11)
+        transposes(14)
+        transposes(15)
+        copy_out(12)
+        copy_out(13)
+        quantise("m", 1, 0)
         scores(0, 0)
-        prepare_mid(1, 0)
-        prepare_mid(1, 1)
         scores(1, 0)
-        prepare_lc(1, 0)
-        prepare_lc(1, 1)
+        copy_out(14)
+        copy_out(15)
+        quantise("m", 1, 1)
+        quantise("l", 1, 0)
+        quantise("l", 1, 1)
         scores(0, 1)
         scores(1, 1)
 
-        for r in range(2):
-            shortcut(nc.vector.tensor_copy, 0, r, 0, C)
-            store(0, r, NA, C)
-        for r in range(2):
-            attention(0, r)
-            store(0, r, 0, NA)
-        for r in range(2):
-            shortcut(nc.scalar.copy, 1, r, NA, C)
-            store(1, r, NA, C)
-        for r in range(2):
-            shortcut(nc.vector.tensor_copy, 1, r, 0, NA)
-            attention(1, r)
-            store(1, r, 0, NA)
+        row_max(0, 0)
+        row_max(1, 0)
+        expand(nc.scalar.copy, 1, 0, 0)
+        expand(nc.scalar.copy, 1, 0, 1)
+        exps(0, 0)
+        exps(1, 0)
+        row_max(0, 1)
+        row_max(1, 1)
+        for m in range(SLOT_ROWS):
+            expand(nc.vector.tensor_copy, 1, 1, m)
+        store_z(1, 1)
+        exps(0, 1)
+        exps(1, 1)
+        expand(nc.scalar.copy, 1, 0, 2)
+        store_z(1, 0)
+        for h in range(H):
+            normalise(h)
+            for r in range(2):
+                region_a(h, r)

@@ -19,9 +19,8 @@ NA = 256
 COLS = 6
 SCALE = 10.0
 ROW = NA * COLS
-SLOT_ROWS = (C - NA) // NA
-SLOTS = 2
-NZ = SLOTS * SLOT_ROWS + 1
+SLOT_ROWS = C // NA
+NZ = SLOT_ROWS + 1
 
 FLOPS = 2 * 2 * 512 * 256 * 2048
 BYTES = 2 * (B * C * 2 * 2) + B * C * 4 * 2 + 2 * (B * C * 2 * 2) + 2 * (B * C * COLS * 4)
@@ -46,10 +45,10 @@ def tile_contextualattention_kernel(tc, left, right, mid, sc00, sc01, sc10, sc11
 
         mid_sb = [keep.tile([P, C * 4], BF16, name="mid%d" % h) for h in range(H)]
         lc_sb = [[keep.tile([P, C * 2], BF16, name="lc%d%d" % (i, h)) for h in range(H)] for i in range(2)]
-        sca = [[keep.tile([P, ROW], BF16, name="sca%d%d" % (h, r)) for r in range(2)] for h in range(H)]
-        scz = keep.tile([P, (NZ + SLOTS * SLOT_ROWS) * ROW], BF16, name="scz")
-        grid = scz[:].rearrange("p (n g) -> p n g", g=ROW)
-        zt = [[keep.tile([P, SLOT_ROWS * ROW], F32, name="zt%d%d" % (h, r)) for r in range(2)] for h in range(H)]
+        xs = keep.tile([P, 2, NA], F32, name="xs")
+        scz = [keep.tile([P, (NZ + SLOT_ROWS) * ROW], BF16, name="scz%d" % r) for r in range(2)]
+        grid = [scz[r][:].rearrange("p (n g) -> p n g", g=ROW) for r in range(2)]
+        zt = [[keep.tile([P, (SLOT_ROWS - 1) * ROW], F32, name="zt%d%d" % (h, r)) for r in range(2)] for h in range(H)]
         at = [[keep.tile([P, ROW], F32, name="at%d%d" % (h, r)) for r in range(2)] for h in range(H)]
         w_sb = [keep.tile([P, COLS, NA], F32, name="w%d" % h) for h in range(H)]
 
@@ -57,8 +56,7 @@ def tile_contextualattention_kernel(tc, left, right, mid, sc00, sc01, sc10, sc11
             return ap[h * P : (h + 1) * P, lo:hi, :].rearrange("b c j -> b (c j)")
 
         def load_z(h, r):
-            lo = (NZ + r * SLOT_ROWS) * ROW
-            nc.sync.dma_start(out=scz[:, lo : lo + SLOT_ROWS * ROW], in_=rows(scs[r], h, NA, C))
+            nc.sync.dma_start(out=scz[r][:, NZ * ROW :], in_=rows(scs[r], h, 0, C))
 
         load_z(0, 0)
         load_z(0, 1)
@@ -68,22 +66,19 @@ def tile_contextualattention_kernel(tc, left, right, mid, sc00, sc01, sc10, sc11
         nc.sync.dma_start(out=mid_sb[1][:], in_=rows(mid, 1, 0, C))
         nc.sync.dma_start(out=lc_sb[1][0][:], in_=rows(right, 0, 0, C))
         nc.sync.dma_start(out=lc_sb[1][1][:], in_=rows(right, 1, 0, C))
-        for h in range(H):
-            for r in range(2):
-                nc.sync.dma_start(out=sca[h][r][:], in_=rows(scs[r], h, 0, NA))
 
         warm = keep.tile([P, 1], F32, name="warm")
         warm2 = keep.tile([P, 1], F32, name="warm2")
         nc.vector.memset(warm[:], 0.0)
         nc.scalar.activation(out=warm2[:], in_=warm[:], func=ACT.Exp)
-        nc.vector.memset(scz[:, : NZ * ROW].bitcast(F32), 0.0)
+        for r in range(2):
+            nc.vector.memset(scz[r][:, : NZ * ROW].bitcast(F32), 0.0)
 
         def expand(copy, h, r, m):
-            q = r * SLOT_ROWS + m
-            n0 = NZ + q
-            k = q + 1
-            src = grid[:, n0 - 2 * k : n0 + 1 : k, :].rearrange("p t (c j) -> p c j t", j=COLS)[:, :, 0:2, :]
-            dst = zt[h][r][:, m * ROW : (m + 1) * ROW].rearrange("p (c i t) -> p c i t", i=2, t=3)
+            n0 = NZ + m
+            k = m + 1
+            src = grid[r][:, n0 - 2 * k : n0 + 1 : k, :].rearrange("p t (c j) -> p c j t", j=COLS)[:, :, 0:2, :]
+            dst = zt[h][r][:, (m - 1) * ROW : m * ROW].rearrange("p (c i t) -> p c i t", i=2, t=3)
             copy(out=dst, in_=src)
 
         def store_z(h, r):
@@ -92,10 +87,17 @@ def tile_contextualattention_kernel(tc, left, right, mid, sc00, sc01, sc10, sc11
         def store_a(h, r):
             nc.sync.dma_start(out=rows(outs[r], h, 0, NA), in_=at[h][r][:])
 
+        def shortcut_planes(h):
+            return w_sb[h][:].rearrange("p (i t) o -> p i t o", t=3)[:, :, 2, :]
+
+        def cast_shortcut(dst, r):
+            src = grid[r][:, NZ, :].rearrange("p (o j) -> p j o", j=COLS)[:, 0:2, :]
+            nc.vector.tensor_copy(out=dst, in_=src)
+
         for r in range(2):
-            for m in range(SLOT_ROWS):
+            cast_shortcut(shortcut_planes(0) if r == 0 else xs[:], r)
+            for m in range(1, SLOT_ROWS):
                 expand(nc.vector.tensor_copy, 0, r, m)
-        for r in range(2):
             load_z(1, r)
         for r in range(2):
             store_z(0, r)
@@ -222,10 +224,10 @@ def tile_contextualattention_kernel(tc, left, right, mid, sc00, sc01, sc10, sc11
                     )
 
         def region_a(h, r):
-            nc.vector.tensor_copy(
-                out=w_sb[h][:].rearrange("p (i t) o -> p i t o", t=3)[:, :, 2, :],
-                in_=sca[h][r][:].rearrange("p (o j) -> p j o", j=COLS)[:, 0:2, :],
-            )
+            if h == 1:
+                cast_shortcut(shortcut_planes(1), r)
+            elif r == 1:
+                nc.vector.tensor_copy(out=shortcut_planes(0), in_=xs[:])
             nc.vector.tensor_copy(
                 out=at[h][r][:].rearrange("p (o j) -> p o j", j=COLS),
                 in_=w_sb[h][:].rearrange("p j o -> p o j"),
@@ -275,21 +277,15 @@ def tile_contextualattention_kernel(tc, left, right, mid, sc00, sc01, sc10, sc11
         scores(0, 1)
         scores(1, 1)
 
-        row_max(0, 0)
-        row_max(1, 0)
-        expand(nc.scalar.copy, 1, 0, 0)
-        expand(nc.scalar.copy, 1, 0, 1)
-        exps(0, 0)
-        exps(1, 0)
-        row_max(0, 1)
-        row_max(1, 1)
-        for m in range(SLOT_ROWS):
+        for m in range(1, SLOT_ROWS):
             expand(nc.vector.tensor_copy, 1, 1, m)
+            expand(nc.scalar.copy, 1, 0, m)
         store_z(1, 1)
-        exps(0, 1)
-        exps(1, 1)
-        expand(nc.scalar.copy, 1, 0, 2)
         store_z(1, 0)
+        for h in range(H):
+            for i in range(2):
+                row_max(h, i)
+                exps(h, i)
         for h in range(H):
             normalise(h)
             for r in range(2):

@@ -14,24 +14,26 @@ ACT = mybir.ActivationFunctionType
 P = 128
 B = 256
 C = 1024
-H = B // P
-NA = 256
-COLS = 6
-SCALE = 10.0
-ROW = NA * COLS
-SLOT_ROWS = C // NA
-NZ = SLOT_ROWS + 1
+HALVES = B // P
+POSITIONS = 6
+STRIP = B * POSITIONS
+SLOT_STRIPS = C * POSITIONS // STRIP
+ZERO_STRIPS = SLOT_STRIPS + 1
+PACK = 4
+K_PASS = P * PACK
+PASSES = C // K_PASS
+UNIT_WORDS = 512
+SOFTMAX_SCALE = 10.0
+AHEAD = 2
 
-FLOPS = 2 * 2 * 512 * 256 * 2048
-BYTES = 2 * (B * C * 2 * 2) + B * C * 4 * 2 + 2 * (B * C * 2 * 2) + 2 * (B * C * COLS * 4)
-
-COPY_ENGINE = "SSSSVVVSSSSSVVVS"
+FLOPS = 2 * 2 * (2 * B) * B * (2 * C)
+BYTES = 2 * (B * C * 2 * 2) + B * C * 4 * 2 + 2 * (B * C * 2 * 2) + 2 * (B * C * POSITIONS * 4)
 
 
 def tile_contextualattention_kernel(tc, left, right, mid, sc00, sc01, sc10, sc11, out_0, out_1):
     nc = tc.nc
     outs = (out_0, out_1)
-    scs = (sc00, sc10)
+    shortcuts = (sc00, sc10)
     with ExitStack() as ctx:
         keep = ctx.enter_context(tc.tile_pool(name="keep", bufs=1))
         stage = ctx.enter_context(tc.tile_pool(name="stage", bufs=3))
@@ -43,250 +45,220 @@ def tile_contextualattention_kernel(tc, left, right, mid, sc00, sc01, sc10, sc11
 
         ctx.enter_context(tc.manual_schedule())
 
-        mid_sb = [keep.tile([P, C * 4], BF16, name="mid%d" % h) for h in range(H)]
-        lc_sb = [[keep.tile([P, C * 2], BF16, name="lc%d%d" % (i, h)) for h in range(H)] for i in range(2)]
-        xs = keep.tile([P, 2, NA], F32, name="xs")
-        scz = [keep.tile([P, (NZ + SLOT_ROWS) * ROW], BF16, name="scz%d" % r) for r in range(2)]
-        grid = [scz[r][:].rearrange("p (n g) -> p n g", g=ROW) for r in range(2)]
-        zt = [[keep.tile([P, (SLOT_ROWS - 1) * ROW], F32, name="zt%d%d" % (h, r)) for r in range(2)] for h in range(H)]
-        at = [[keep.tile([P, ROW], F32, name="at%d%d" % (h, r)) for r in range(2)] for h in range(H)]
-        w_sb = [keep.tile([P, COLS, NA], F32, name="w%d" % h) for h in range(H)]
+        mid_sb = [keep.tile([P, C * 4], BF16, name="mid%d" % h) for h in range(HALVES)]
+        lc_sb = [[keep.tile([P, C * 2], BF16, name="lc%d%d" % (i, ho)) for ho in range(HALVES)] for i in range(2)]
+        padded = [keep.tile([P, (ZERO_STRIPS + SLOT_STRIPS) * STRIP], BF16, name="padded%d" % r) for r in range(2)]
+        strips = [padded[r][:].rearrange("p (n x) -> p n x", x=STRIP) for r in range(2)]
+        kept = [keep.tile([P, 2, B], BF16, name="kept%d" % r) for r in range(2)]
+        tail_out = [
+            [keep.tile([P, (SLOT_STRIPS - 1) * STRIP], F32, name="tail%d%d" % (h, r)) for r in range(2)]
+            for h in range(HALVES)
+        ]
+        head_out = [[keep.tile([P, STRIP], F32, name="head%d%d" % (h, r)) for r in range(2)] for h in range(HALVES)]
+        planes = [keep.tile([P, POSITIONS, B], F32, name="planes%d" % h) for h in range(HALVES)]
 
-        def rows(ap, h, lo, hi):
-            return ap[h * P : (h + 1) * P, lo:hi, :].rearrange("b c j -> b (c j)")
+        def dram_rows(ap, h, first_channel, end_channel):
+            return ap[h * P : (h + 1) * P, first_channel:end_channel, :].rearrange("b c j -> b (c j)")
 
-        def load_z(h, r):
-            nc.sync.dma_start(out=scz[r][:, NZ * ROW :], in_=rows(scs[r], h, 0, C))
+        def load_slot(h, r):
+            nc.sync.dma_start(out=padded[r][:, ZERO_STRIPS * STRIP :], in_=dram_rows(shortcuts[r], h, 0, C))
 
-        load_z(0, 0)
-        load_z(0, 1)
-        nc.sync.dma_start(out=mid_sb[0][:], in_=rows(mid, 0, 0, C))
-        nc.sync.dma_start(out=lc_sb[0][0][:], in_=rows(left, 0, 0, C))
-        nc.sync.dma_start(out=lc_sb[0][1][:], in_=rows(left, 1, 0, C))
-        nc.sync.dma_start(out=mid_sb[1][:], in_=rows(mid, 1, 0, C))
-        nc.sync.dma_start(out=lc_sb[1][0][:], in_=rows(right, 0, 0, C))
-        nc.sync.dma_start(out=lc_sb[1][1][:], in_=rows(right, 1, 0, C))
+        load_slot(0, 0)
+        load_slot(0, 1)
+        nc.sync.dma_start(out=mid_sb[0][:], in_=dram_rows(mid, 0, 0, C))
+        nc.sync.dma_start(out=lc_sb[0][0][:], in_=dram_rows(left, 0, 0, C))
+        nc.sync.dma_start(out=lc_sb[0][1][:], in_=dram_rows(left, 1, 0, C))
+        nc.sync.dma_start(out=mid_sb[1][:], in_=dram_rows(mid, 1, 0, C))
+        nc.sync.dma_start(out=lc_sb[1][0][:], in_=dram_rows(right, 0, 0, C))
+        nc.sync.dma_start(out=lc_sb[1][1][:], in_=dram_rows(right, 1, 0, C))
 
-        warm = keep.tile([P, 1], F32, name="warm")
-        warm2 = keep.tile([P, 1], F32, name="warm2")
-        nc.vector.memset(warm[:], 0.0)
-        nc.scalar.activation(out=warm2[:], in_=warm[:], func=ACT.Exp)
+        warm_in = keep.tile([P, 1], F32, name="warm_in")
+        warm_out = keep.tile([P, 1], F32, name="warm_out")
+        nc.vector.memset(warm_in[:], 0.0)
+        nc.scalar.activation(out=warm_out[:], in_=warm_in[:], func=ACT.Exp)
         for r in range(2):
-            nc.vector.memset(scz[r][:, : NZ * ROW].bitcast(F32), 0.0)
+            nc.vector.memset(padded[r][:, : ZERO_STRIPS * STRIP].bitcast(F32), 0.0)
 
         def expand(copy, h, r, m):
-            n0 = NZ + m
-            k = m + 1
-            src = grid[r][:, n0 - 2 * k : n0 + 1 : k, :].rearrange("p t (c j) -> p c j t", j=COLS)[:, :, 0:2, :]
-            dst = zt[h][r][:, (m - 1) * ROW : m * ROW].rearrange("p (c i t) -> p c i t", i=2, t=3)
+            last = ZERO_STRIPS + m
+            step = m + 1
+            src = strips[r][:, last - 2 * step : last + 1 : step, :]
+            src = src.rearrange("p t (c j) -> p c j t", j=POSITIONS)[:, :, 0:2, :]
+            dst = tail_out[h][r][:, (m - 1) * STRIP : m * STRIP].rearrange("p (c i t) -> p c i t", i=2, t=3)
             copy(out=dst, in_=src)
 
-        def store_z(h, r):
-            nc.sync.dma_start(out=rows(outs[r], h, NA, C), in_=zt[h][r][:])
+        def first_strip_shortcuts(r):
+            return strips[r][:, ZERO_STRIPS, :].rearrange("p (o j) -> p j o", j=POSITIONS)[:, 0:2, :]
 
-        def store_a(h, r):
-            nc.sync.dma_start(out=rows(outs[r], h, 0, NA), in_=at[h][r][:])
+        def store_tail(h, r):
+            nc.sync.dma_start(out=dram_rows(outs[r], h, B, C), in_=tail_out[h][r][:])
 
-        def shortcut_planes(h):
-            return w_sb[h][:].rearrange("p (i t) o -> p i t o", t=3)[:, :, 2, :]
-
-        def cast_shortcut(dst, r):
-            src = grid[r][:, NZ, :].rearrange("p (o j) -> p j o", j=COLS)[:, 0:2, :]
-            nc.vector.tensor_copy(out=dst, in_=src)
+        def store_head(h, r):
+            nc.sync.dma_start(out=dram_rows(outs[r], h, 0, B), in_=head_out[h][r][:])
 
         for r in range(2):
-            cast_shortcut(shortcut_planes(0) if r == 0 else xs[:], r)
-            for m in range(1, SLOT_ROWS):
+            nc.vector.tensor_copy(out=kept[r][:], in_=first_strip_shortcuts(r))
+            for m in range(1, SLOT_STRIPS):
                 expand(nc.vector.tensor_copy, 0, r, m)
-            load_z(1, r)
+            load_slot(1, r)
         for r in range(2):
-            store_z(0, r)
+            store_tail(0, r)
 
-        m_codes = keep.tile([P, 2048], U32, name="m_codes", align_bytes=64)
-        m_scales = keep.tile([P, 2048], U8, name="m_scales", align_bytes=64)
-        l_codes = keep.tile([P, 2048], U32, name="l_codes", align_bytes=64)
-        l_scales = keep.tile([P, 2048], U8, name="l_scales", align_bytes=64)
+        mid_words = keep.tile([P, 4 * UNIT_WORDS], U32, name="mid_words", align_bytes=64)
+        mid_scales = keep.tile([P, 4 * UNIT_WORDS], U8, name="mid_scales", align_bytes=64)
+        lc_words = keep.tile([P, 4 * UNIT_WORDS], U32, name="lc_words", align_bytes=64)
+        lc_scales = keep.tile([P, 4 * UNIT_WORDS], U8, name="lc_scales", align_bytes=64)
 
-        banks = []
-        for first in range(2):
-            for i in range(2):
-                for g in range(2):
-                    banks.append(("m", first, i, g))
-            for g in range(2):
-                for ho in range(2):
-                    banks.append(("l", first, g, ho))
+        units = []
+        for x in range(2):
+            units.extend([("mid", x, 0), ("mid", x, 1), ("lc", x, 0), ("lc", x, 1)])
         bank_tiles = {}
-        grouped_tiles = {}
+        column_tiles = {}
 
-        def transposes(n):
-            kind, a, b, c = banks[n]
-            bank = psum_t.tile([P, 512], F32, tag="xt", name="xt")
-            bank_tiles[n] = bank
-            for t in range(4):
-                if kind == "m":
-                    c0 = 512 * c + P * t
-                    src = mid_sb[a][:].bitcast(F32).rearrange("b (c i) -> b c i", i=2)[:, c0 : c0 + P, b]
+        def transposes(u):
+            kind, a, b = units[u]
+            for half in range(2):
+                bank = psum_t.tile([P, PACK * P], F32, tag="bank", name="bank")
+                bank_tiles[(u, half)] = bank
+                for v in range(PACK):
+                    if kind == "mid":
+                        c0 = K_PASS * half + P * v
+                        src = mid_sb[a][:].bitcast(F32).rearrange("b (c i) -> b c i", i=2)[:, c0 : c0 + P, b]
+                    else:
+                        c0 = K_PASS * b + P * v
+                        src = lc_sb[a][half][:].bitcast(F32)[:, c0 : c0 + P]
+                    nc.tensor.transpose(bank[:, v * P : (v + 1) * P], src, ident[:])
+
+        def copy_out(u):
+            kind, a, b = units[u]
+            columns = stage.tile([P, 2, 2, P, PACK], BF16, tag="columns", name="columns", align_bytes=64)
+            column_tiles[u] = columns
+            for half in range(2):
+                dst = columns[:, half] if kind == "mid" else columns[:, :, half]
+                src = bank_tiles[(u, half)][:].bitcast(BF16).rearrange("p (v w e) -> p e w v", v=PACK, w=P, e=2)
+                if kind == "lc" and (b, half) != (1, 1):
+                    nc.vector.tensor_copy(out=dst, in_=src)
                 else:
-                    c0 = 512 * b + P * t
-                    src = lc_sb[a][c][:].bitcast(F32)[:, c0 : c0 + P]
-                nc.tensor.transpose(bank[:, t * P : (t + 1) * P], src, ident[:])
+                    nc.scalar.copy(out=dst, in_=src)
 
-        def copy_out(n):
-            kind, a, b, c = banks[n]
-            key = (kind, a, b)
-            if key not in grouped_tiles:
-                grouped_tiles[key] = stage.tile([P, 2, 2, P, 4], BF16, tag="grouped", name="grouped", align_bytes=64)
-            grouped = grouped_tiles[key]
-            dst = grouped[:, c] if kind == "m" else grouped[:, :, c]
-            src = bank_tiles[n][:].bitcast(BF16).rearrange("p (t w e) -> p e w t", t=4, w=P, e=2)
-            if COPY_ENGINE[n] == "V":
-                nc.vector.tensor_copy(out=dst, in_=src)
-            else:
-                nc.scalar.copy(out=dst, in_=src)
-
-        def quantise(kind, a, b):
-            codes, scales = (m_codes, m_scales) if kind == "m" else (l_codes, l_scales)
-            unit = 2 * a + b
-            cols = slice(unit * 512, (unit + 1) * 512)
+        def quantise(u):
+            kind, a, b = units[u]
+            words, scales = (mid_words, mid_scales) if kind == "mid" else (lc_words, lc_scales)
+            cols = slice((2 * a + b) * UNIT_WORDS, (2 * a + b + 1) * UNIT_WORDS)
             nc.vector.quantize_mx(
-                out=codes[:, cols].bitcast(FP8X4),
+                out=words[:, cols].bitcast(FP8X4),
                 scales=scales[:, cols],
-                in_=grouped_tiles[(kind, a, b)][:].rearrange("p a b w t -> p (a b w t)"),
+                in_=column_tiles[u][:].rearrange("p x y w v -> p (x y w v)"),
             )
 
-        mx = keep.tile([P, 8], F32, name="mx")
-        nb = keep.tile([P, 8], F32, name="nb")
-        sm = keep.tile([P, 8], F32, name="sm")
-        rs = keep.tile([P, 8], F32, name="rs")
-        acc_tiles = {}
+        row_maxima = keep.tile([P, 8], F32, name="row_maxima")
+        biases = keep.tile([P, 8], F32, name="biases")
+        sums = keep.tile([P, 8], F32, name="sums")
+        inverse_sums = keep.tile([P, 8], F32, name="inverse_sums")
+        score_tiles = {}
 
-        def m_op(h, i, g, e):
+        def mid_cols(h, i, g, e):
             lo = (((h * 2 + i) * 2 + g) * 2 + e) * P
             return slice(lo, lo + P)
 
-        def l_op(i, g, e):
-            lo = ((i * 2 + g) * 2 + e) * 2 * P
-            return slice(lo, lo + 2 * P)
+        def lc_cols(i, g, e):
+            lo = ((i * 2 + g) * 2 + e) * B
+            return slice(lo, lo + B)
+
+        def last_unit(h, i):
+            return max(units.index(("mid", h, i)), units.index(("lc", i, PASSES - 1)))
 
         def scores(h, i):
-            acc = psum_s.tile([P, 2 * NA], F32, tag="acc", name="acc")
-            acc_tiles[(h, i)] = acc
-            plans = (
-                [(g, 0, 1) for g in range(2)],
-                [(g, e, e) for g in range(2) for e in range(2)],
+            bank = psum_s.tile([P, 2 * B], F32, tag="scores", name="scores")
+            score_tiles[(h, i)] = bank
+            taps = (
+                [(g, 0, 1) for g in range(PASSES)],
+                [(g, e, e) for g in range(PASSES) for e in range(2)],
             )
             for t in range(2):
-                plan = plans[t]
-                for n, (g, em, el) in enumerate(plan):
+                for n, (g, e_mid, e_lc) in enumerate(taps[t]):
                     nc.tensor.matmul_mx(
-                        out=acc[:, t * NA : (t + 1) * NA],
-                        lhsT=m_codes[:, m_op(h, i, g, em)].bitcast(FP8X4),
-                        lhsT_scale=m_scales[:, m_op(h, i, g, em)],
-                        rhs=l_codes[:, l_op(i, g, el)].bitcast(FP8X4),
-                        rhs_scale=l_scales[:, l_op(i, g, el)],
+                        out=bank[:, t * B : (t + 1) * B],
+                        lhsT=mid_words[:, mid_cols(h, i, g, e_mid)].bitcast(FP8X4),
+                        lhsT_scale=mid_scales[:, mid_cols(h, i, g, e_mid)],
+                        rhs=lc_words[:, lc_cols(i, g, e_lc)].bitcast(FP8X4),
+                        rhs_scale=lc_scales[:, lc_cols(i, g, e_lc)],
                         start=(n == 0),
-                        stop=(n == len(plan) - 1),
+                        stop=(n == len(taps[t]) - 1),
                     )
 
-        def row_max(h, i):
-            k = (h * 2 + i) * 2
+        def exponentials(h, i):
+            col = (h * 2 + i) * 2
             nc.vector.tensor_reduce(
-                out=mx[:, k : k + 2],
-                in_=acc_tiles[(h, i)][:].rearrange("p (t o) -> p t o", t=2),
+                out=row_maxima[:, col : col + 2],
+                in_=score_tiles[(h, i)][:].rearrange("p (t o) -> p t o", t=2),
                 axis=mybir.AxisListType.X,
                 op=ALU.max,
             )
-            nc.vector.tensor_scalar(out=nb[:, k : k + 2], in0=mx[:, k : k + 2], scalar1=-SCALE, scalar2=None, op0=ALU.mult)
-
-        def exps(h, i):
-            k = (h * 2 + i) * 2
+            nc.vector.tensor_scalar(
+                out=biases[:, col : col + 2],
+                in0=row_maxima[:, col : col + 2],
+                scalar1=-SOFTMAX_SCALE,
+                scalar2=None,
+                op0=ALU.mult,
+            )
             for t in range(2):
                 nc.scalar.activation(
-                    out=w_sb[h][:, 3 * i + t, :],
-                    in_=acc_tiles[(h, i)][:, t * NA : (t + 1) * NA],
+                    out=planes[h][:, 3 * i + t, :],
+                    in_=score_tiles[(h, i)][:, t * B : (t + 1) * B],
                     func=ACT.Exp,
-                    bias=nb[:, k + t : k + t + 1],
-                    scale=SCALE,
-                    accum_out=sm[:, k + t : k + t + 1],
+                    bias=biases[:, col + t : col + t + 1],
+                    scale=SOFTMAX_SCALE,
+                    accum_out=sums[:, col + t : col + t + 1],
                 )
 
         def normalise(h):
-            nc.vector.reciprocal(out=rs[:, 4 * h : 4 * h + 4], in_=sm[:, 4 * h : 4 * h + 4])
+            nc.vector.reciprocal(out=inverse_sums[:, 4 * h : 4 * h + 4], in_=sums[:, 4 * h : 4 * h + 4])
             for i in range(2):
                 for t in range(2):
-                    k = (h * 2 + i) * 2 + t
+                    col = (h * 2 + i) * 2 + t
                     nc.vector.tensor_scalar(
-                        out=w_sb[h][:, 3 * i + t, :],
-                        in0=w_sb[h][:, 3 * i + t, :],
-                        scalar1=rs[:, k : k + 1],
+                        out=planes[h][:, 3 * i + t, :],
+                        in0=planes[h][:, 3 * i + t, :],
+                        scalar1=inverse_sums[:, col : col + 1],
                         scalar2=None,
                         op0=ALU.mult,
                     )
 
-        def region_a(h, r):
-            if h == 1:
-                cast_shortcut(shortcut_planes(1), r)
-            elif r == 1:
-                nc.vector.tensor_copy(out=shortcut_planes(0), in_=xs[:])
+        def first_strip(h, r):
             nc.vector.tensor_copy(
-                out=at[h][r][:].rearrange("p (o j) -> p o j", j=COLS),
-                in_=w_sb[h][:].rearrange("p j o -> p o j"),
+                out=planes[h][:].rearrange("p (i t) o -> p i t o", t=3)[:, :, 2, :],
+                in_=kept[r][:] if h == 0 else first_strip_shortcuts(r),
             )
-            store_a(h, r)
+            nc.vector.tensor_copy(
+                out=head_out[h][r][:].rearrange("p (o j) -> p o j", j=POSITIONS),
+                in_=planes[h][:].rearrange("p j o -> p o j"),
+            )
+            store_head(h, r)
 
-        for n in (0, 1, 2, 3):
-            transposes(n)
-        copy_out(0)
-        copy_out(1)
-        transposes(4)
-        transposes(5)
-        copy_out(2)
-        copy_out(3)
-        transposes(6)
-        transposes(7)
-        copy_out(4)
-        copy_out(5)
-        transposes(8)
-        transposes(9)
-        quantise("m", 0, 0)
-        quantise("m", 0, 1)
-        copy_out(6)
-        copy_out(7)
-        transposes(10)
-        transposes(11)
-        quantise("l", 0, 0)
-        copy_out(8)
-        copy_out(9)
-        transposes(12)
-        transposes(13)
-        quantise("l", 0, 1)
-        copy_out(10)
-        copy_out(11)
-        transposes(14)
-        transposes(15)
-        copy_out(12)
-        copy_out(13)
-        quantise("m", 1, 0)
-        scores(0, 0)
-        scores(1, 0)
-        copy_out(14)
-        copy_out(15)
-        quantise("m", 1, 1)
-        quantise("l", 1, 0)
-        quantise("l", 1, 1)
-        scores(0, 1)
-        scores(1, 1)
+        for u in range(AHEAD):
+            transposes(u)
+        for u in range(len(units) + 1):
+            if u < len(units):
+                copy_out(u)
+            if u + AHEAD < len(units):
+                transposes(u + AHEAD)
+            if u >= 1:
+                quantise(u - 1)
+                for h in range(HALVES):
+                    for i in range(2):
+                        if last_unit(h, i) == u - 1:
+                            scores(h, i)
 
-        for m in range(1, SLOT_ROWS):
+        for m in range(1, SLOT_STRIPS):
             expand(nc.vector.tensor_copy, 1, 1, m)
             expand(nc.scalar.copy, 1, 0, m)
-        store_z(1, 1)
-        store_z(1, 0)
-        for h in range(H):
+        store_tail(1, 1)
+        store_tail(1, 0)
+        for h in range(HALVES):
             for i in range(2):
-                row_max(h, i)
-                exps(h, i)
-        for h in range(H):
+                exponentials(h, i)
+        for h in range(HALVES):
             normalise(h)
             for r in range(2):
-                region_a(h, r)
+                first_strip(h, r)

@@ -45,16 +45,16 @@ def tile_contextualattention_kernel(tc, left, right, mid, sc00, sc01, sc10, sc11
 
         ctx.enter_context(tc.manual_schedule())
 
-        mid_sb = [keep.tile([P, C * 4], BF16, name="mid%d" % h) for h in range(HALVES)]
-        lc_sb = [[keep.tile([P, C * 2], BF16, name="lc%d%d" % (i, ho)) for ho in range(HALVES)] for i in range(2)]
-        padded = [keep.tile([P, (ZERO_STRIPS + SLOT_STRIPS) * STRIP], BF16, name="padded%d" % r) for r in range(2)]
+        mid_sb = [keep.tile([P, C * 4], BF16, name="mid%d" % h, align_bytes=256) for h in range(HALVES)]
+        lc_sb = [[keep.tile([P, C * 2], BF16, name="lc%d%d" % (i, ho), align_bytes=256) for ho in range(HALVES)] for i in range(2)]
+        padded = [keep.tile([P, (ZERO_STRIPS + SLOT_STRIPS) * STRIP], BF16, name="padded%d" % r, align_bytes=256) for r in range(2)]
         strips = [padded[r][:].rearrange("p (n x) -> p n x", x=STRIP) for r in range(2)]
         kept = [keep.tile([P, 2, B], BF16, name="kept%d" % r) for r in range(2)]
         tail_out = [
-            [keep.tile([P, (SLOT_STRIPS - 1) * STRIP], F32, name="tail%d%d" % (h, r)) for r in range(2)]
+            [keep.tile([P, (SLOT_STRIPS - 1) * STRIP], F32, name="tail%d%d" % (h, r), align_bytes=256) for r in range(2)]
             for h in range(HALVES)
         ]
-        head_out = [[keep.tile([P, STRIP], F32, name="head%d%d" % (h, r)) for r in range(2)] for h in range(HALVES)]
+        head_out = [[keep.tile([P, STRIP], F32, name="head%d%d" % (h, r), align_bytes=256) for r in range(2)] for h in range(HALVES)]
         planes = [keep.tile([P, POSITIONS, B], F32, name="planes%d" % h) for h in range(HALVES)]
 
         def dram_rows(ap, h, first_channel, end_channel):

@@ -45,8 +45,8 @@ def tile_contextualattention_kernel(tc, left, right, mid, sc00, sc01, sc10, sc11
 
         ctx.enter_context(tc.manual_schedule())
 
-        mid_sb = [keep.tile([P, C * 4], BF16, name="mid%d" % h, align_bytes=256) for h in range(HALVES)]
-        lc_sb = [[keep.tile([P, C * 2], BF16, name="lc%d%d" % (i, ho), align_bytes=256) for ho in range(HALVES)] for i in range(2)]
+        mid_sb = keep.tile([P, HALVES * C * 4], BF16, name="mid_sb", align_bytes=256)
+        lc_sb = [keep.tile([P, HALVES * C * 2], BF16, name="lc%d" % i, align_bytes=256) for i in range(2)]
         padded = [keep.tile([P, (ZERO_STRIPS + SLOT_STRIPS) * STRIP], BF16, name="padded%d" % r, align_bytes=256) for r in range(2)]
         strips = [padded[r][:].rearrange("p (n x) -> p n x", x=STRIP) for r in range(2)]
         kept = [keep.tile([P, 2, B], BF16, name="kept%d" % r) for r in range(2)]
@@ -54,23 +54,23 @@ def tile_contextualattention_kernel(tc, left, right, mid, sc00, sc01, sc10, sc11
             [keep.tile([P, (SLOT_STRIPS - 1) * STRIP], F32, name="tail%d%d" % (h, r), align_bytes=256) for r in range(2)]
             for h in range(HALVES)
         ]
-        head_out = [[keep.tile([P, STRIP], F32, name="head%d%d" % (h, r), align_bytes=256) for r in range(2)] for h in range(HALVES)]
+        head_out = [keep.tile([P, HALVES, STRIP], F32, name="head%d" % r, align_bytes=256) for r in range(2)]
         planes = [keep.tile([P, POSITIONS, B], F32, name="planes%d" % h) for h in range(HALVES)]
 
         def dram_rows(ap, h, first_channel, end_channel):
-            return ap[h * P : (h + 1) * P, first_channel:end_channel, :].rearrange("b c j -> b (c j)")
+            return ap.rearrange("(p h) c j -> p h c j", h=HALVES)[:, h, first_channel:end_channel, :].rearrange("p c j -> p (c j)")
+
+        def both_rows(ap):
+            return ap.rearrange("(p h) c j -> p (h c j)", h=HALVES)
 
         def load_slot(h, r):
             nc.sync.dma_start(out=padded[r][:, ZERO_STRIPS * STRIP :], in_=dram_rows(shortcuts[r], h, 0, C))
 
         load_slot(0, 0)
         load_slot(0, 1)
-        nc.sync.dma_start(out=mid_sb[0][:], in_=dram_rows(mid, 0, 0, C))
-        nc.sync.dma_start(out=lc_sb[0][0][:], in_=dram_rows(left, 0, 0, C))
-        nc.sync.dma_start(out=lc_sb[0][1][:], in_=dram_rows(left, 1, 0, C))
-        nc.sync.dma_start(out=mid_sb[1][:], in_=dram_rows(mid, 1, 0, C))
-        nc.sync.dma_start(out=lc_sb[1][0][:], in_=dram_rows(right, 0, 0, C))
-        nc.sync.dma_start(out=lc_sb[1][1][:], in_=dram_rows(right, 1, 0, C))
+        nc.sync.dma_start(out=mid_sb[:], in_=both_rows(mid))
+        nc.sync.dma_start(out=lc_sb[0][:], in_=both_rows(left))
+        nc.sync.dma_start(out=lc_sb[1][:], in_=both_rows(right))
 
         warm_in = keep.tile([P, 1], F32, name="warm_in")
         warm_out = keep.tile([P, 1], F32, name="warm_out")
@@ -93,8 +93,10 @@ def tile_contextualattention_kernel(tc, left, right, mid, sc00, sc01, sc10, sc11
         def store_tail(h, r):
             nc.sync.dma_start(out=dram_rows(outs[r], h, B, C), in_=tail_out[h][r][:])
 
-        def store_head(h, r):
-            nc.sync.dma_start(out=dram_rows(outs[r], h, 0, B), in_=head_out[h][r][:])
+        def store_heads(r):
+            nc.sync.dma_start(
+                out=outs[r].rearrange("(p h) c j -> p h (c j)", h=HALVES)[:, :, :STRIP], in_=head_out[r][:]
+            )
 
         for r in range(2):
             nc.vector.tensor_copy(out=kept[r][:], in_=first_strip_shortcuts(r))
@@ -109,9 +111,7 @@ def tile_contextualattention_kernel(tc, left, right, mid, sc00, sc01, sc10, sc11
         lc_words = keep.tile([P, 4 * UNIT_WORDS], U32, name="lc_words", align_bytes=64)
         lc_scales = keep.tile([P, 4 * UNIT_WORDS], U8, name="lc_scales", align_bytes=64)
 
-        units = []
-        for x in range(2):
-            units.extend([("mid", x, 0), ("mid", x, 1), ("lc", x, 0), ("lc", x, 1)])
+        units = [(kind, x, y) for kind in ("mid", "lc") for x in range(2) for y in range(2)]
         bank_tiles = {}
         column_tiles = {}
 
@@ -122,11 +122,11 @@ def tile_contextualattention_kernel(tc, left, right, mid, sc00, sc01, sc10, sc11
                 bank_tiles[(u, half)] = bank
                 for v in range(PACK):
                     if kind == "mid":
-                        c0 = K_PASS * half + P * v
-                        src = mid_sb[a][:].bitcast(F32).rearrange("b (c i) -> b c i", i=2)[:, c0 : c0 + P, b]
+                        c0 = a * C + K_PASS * half + P * v
+                        src = mid_sb[:].bitcast(F32).rearrange("b (c i) -> b c i", i=2)[:, c0 : c0 + P, b]
                     else:
-                        c0 = K_PASS * b + P * v
-                        src = lc_sb[a][half][:].bitcast(F32)[:, c0 : c0 + P]
+                        c0 = half * C + K_PASS * b + P * v
+                        src = lc_sb[a][:].bitcast(F32)[:, c0 : c0 + P]
                     nc.tensor.transpose(bank[:, v * P : (v + 1) * P], src, ident[:])
 
         def copy_out(u):
@@ -136,7 +136,7 @@ def tile_contextualattention_kernel(tc, left, right, mid, sc00, sc01, sc10, sc11
             for half in range(2):
                 dst = columns[:, half] if kind == "mid" else columns[:, :, half]
                 src = bank_tiles[(u, half)][:].bitcast(BF16).rearrange("p (v w e) -> p e w v", v=PACK, w=P, e=2)
-                if kind == "lc" and (b, half) != (1, 1):
+                if half == 1 and (a, b) != (1, 1):
                     nc.vector.tensor_copy(out=dst, in_=src)
                 else:
                     nc.scalar.copy(out=dst, in_=src)
@@ -204,8 +204,8 @@ def tile_contextualattention_kernel(tc, left, right, mid, sc00, sc01, sc10, sc11
             )
             for t in range(2):
                 nc.scalar.activation(
-                    out=planes[h][:, 3 * i + t, :],
-                    in_=score_tiles[(h, i)][:, t * B : (t + 1) * B],
+                    out=planes[h][:, 3 * i + t, :].rearrange("p (w ho) -> p w ho", ho=HALVES),
+                    in_=score_tiles[(h, i)][:, t * B : (t + 1) * B].rearrange("p (ho w) -> p w ho", ho=HALVES),
                     func=ACT.Exp,
                     bias=biases[:, col + t : col + t + 1],
                     scale=SOFTMAX_SCALE,
@@ -231,10 +231,9 @@ def tile_contextualattention_kernel(tc, left, right, mid, sc00, sc01, sc10, sc11
                 in_=kept[r][:] if h == 0 else first_strip_shortcuts(r),
             )
             nc.vector.tensor_copy(
-                out=head_out[h][r][:].rearrange("p (o j) -> p o j", j=POSITIONS),
+                out=head_out[r][:, h, :].rearrange("p (o j) -> p o j", j=POSITIONS),
                 in_=planes[h][:].rearrange("p j o -> p o j"),
             )
-            store_head(h, r)
 
         for u in range(AHEAD):
             transposes(u)
@@ -260,5 +259,8 @@ def tile_contextualattention_kernel(tc, left, right, mid, sc00, sc01, sc10, sc11
                 exponentials(h, i)
         for h in range(HALVES):
             normalise(h)
-            for r in range(2):
-                first_strip(h, r)
+            first_strip(h, 0)
+        store_heads(0)
+        for h in range(HALVES):
+            first_strip(h, 1)
+        store_heads(1)

@@ -17,8 +17,10 @@ C = 1024
 HALVES = B // P
 POSITIONS = 6
 STRIP = B * POSITIONS
-SLOT_STRIPS = C * POSITIONS // STRIP
-ZERO_STRIPS = SLOT_STRIPS + 1
+ROW_STRIPS = C * POSITIONS // STRIP
+SHORTCUT_STRIPS = 2 * HALVES * ROW_STRIPS
+ZERO_STRIPS = SHORTCUT_STRIPS + 1
+VECTOR_ZERO_STRIPS = 12
 PACK = 4
 K_PASS = P * PACK
 PASSES = C // K_PASS
@@ -45,17 +47,17 @@ def tile_contextualattention_kernel(tc, left, right, mid, sc00, sc01, sc10, sc11
 
         ctx.enter_context(tc.manual_schedule())
 
-        mid_sb = keep.tile([P, HALVES * C * 4], BF16, name="mid_sb", align_bytes=256)
-        lc_sb = [keep.tile([P, HALVES * C * 2], BF16, name="lc%d" % i, align_bytes=256) for i in range(2)]
-        padded = [keep.tile([P, (ZERO_STRIPS + SLOT_STRIPS) * STRIP], BF16, name="padded%d" % r, align_bytes=256) for r in range(2)]
-        strips = [padded[r][:].rearrange("p (n x) -> p n x", x=STRIP) for r in range(2)]
-        kept = [keep.tile([P, 2, B], BF16, name="kept%d" % r) for r in range(2)]
-        tail_out = [
-            [keep.tile([P, (SLOT_STRIPS - 1) * STRIP], F32, name="tail%d%d" % (h, r), align_bytes=256) for r in range(2)]
-            for h in range(HALVES)
+        mid_sb = keep.tile([P, HALVES * C * 4], BF16, tag="mid_then_head0", name="mid_sb", align_bytes=256)
+        lc_sb = [
+            keep.tile([P, HALVES * C * 2], BF16, tag="lc_then_planes%d" % i, name="lc%d" % i, align_bytes=256)
+            for i in range(2)
         ]
-        head_out = [keep.tile([P, HALVES, STRIP], F32, name="head%d" % r, align_bytes=256) for r in range(2)]
-        planes = [keep.tile([P, POSITIONS, B], F32, name="planes%d" % h) for h in range(HALVES)]
+        padded = keep.tile([P, (ZERO_STRIPS + SHORTCUT_STRIPS) * STRIP], BF16, name="padded", align_bytes=256)
+        strips = padded[:].rearrange("p (n x) -> p n x", x=STRIP)
+        tail_out = [
+            keep.tile([P, HALVES, (ROW_STRIPS - 1) * STRIP], F32, tag=tag, name="tail", align_bytes=256)
+            for tag in ("tail0_then_head1", "tail1")
+        ]
 
         def dram_rows(ap, h, first_channel, end_channel):
             return ap.rearrange("(p h) c j -> p h c j", h=HALVES)[:, h, first_channel:end_channel, :].rearrange("p c j -> p (c j)")
@@ -63,48 +65,49 @@ def tile_contextualattention_kernel(tc, left, right, mid, sc00, sc01, sc10, sc11
         def both_rows(ap):
             return ap.rearrange("(p h) c j -> p (h c j)", h=HALVES)
 
-        def load_slot(h, r):
-            nc.sync.dma_start(out=padded[r][:, ZERO_STRIPS * STRIP :], in_=dram_rows(shortcuts[r], h, 0, C))
+        def load_shortcuts(r):
+            first = ZERO_STRIPS + r * HALVES * ROW_STRIPS
+            nc.sync.dma_start(
+                out=padded[:, first * STRIP : (first + HALVES * ROW_STRIPS) * STRIP], in_=both_rows(shortcuts[r])
+            )
 
-        load_slot(0, 0)
-        load_slot(0, 1)
+        load_shortcuts(0)
         nc.sync.dma_start(out=mid_sb[:], in_=both_rows(mid))
         nc.sync.dma_start(out=lc_sb[0][:], in_=both_rows(left))
         nc.sync.dma_start(out=lc_sb[1][:], in_=both_rows(right))
+        load_shortcuts(1)
 
         warm_in = keep.tile([P, 1], F32, name="warm_in")
         warm_out = keep.tile([P, 1], F32, name="warm_out")
         nc.vector.memset(warm_in[:], 0.0)
         nc.scalar.activation(out=warm_out[:], in_=warm_in[:], func=ACT.Exp)
-        for r in range(2):
-            nc.vector.memset(padded[r][:, : ZERO_STRIPS * STRIP].bitcast(F32), 0.0)
+        nc.vector.memset(padded[:, : VECTOR_ZERO_STRIPS * STRIP].bitcast(F32), 0.0)
+        nc.gpsimd.memset(padded[:, VECTOR_ZERO_STRIPS * STRIP : ZERO_STRIPS * STRIP].bitcast(F32), 0.0)
 
         def expand(copy, h, r, m):
-            last = ZERO_STRIPS + m
-            step = m + 1
-            src = strips[r][:, last - 2 * step : last + 1 : step, :]
+            n = (r * HALVES + h) * ROW_STRIPS + m
+            last = ZERO_STRIPS + n
+            step = n + 1
+            src = strips[:, last - 2 * step : last + 1 : step, :]
             src = src.rearrange("p t (c j) -> p c j t", j=POSITIONS)[:, :, 0:2, :]
-            dst = tail_out[h][r][:, (m - 1) * STRIP : m * STRIP].rearrange("p (c i t) -> p c i t", i=2, t=3)
+            dst = tail_out[r][:, h, (m - 1) * STRIP : m * STRIP].rearrange("p (c i t) -> p c i t", i=2, t=3)
             copy(out=dst, in_=src)
 
-        def first_strip_shortcuts(r):
-            return strips[r][:, ZERO_STRIPS, :].rearrange("p (o j) -> p j o", j=POSITIONS)[:, 0:2, :]
-
-        def store_tail(h, r):
-            nc.sync.dma_start(out=dram_rows(outs[r], h, B, C), in_=tail_out[h][r][:])
+        def first_strip_shortcuts(h, r):
+            row = strips[:, ZERO_STRIPS + (r * HALVES + h) * ROW_STRIPS, :]
+            return row.rearrange("p (o j) -> p j o", j=POSITIONS)[:, 0:2, :]
 
         def store_heads(r):
             nc.sync.dma_start(
                 out=outs[r].rearrange("(p h) c j -> p h (c j)", h=HALVES)[:, :, :STRIP], in_=head_out[r][:]
             )
 
-        for r in range(2):
-            nc.vector.tensor_copy(out=kept[r][:], in_=first_strip_shortcuts(r))
-            for m in range(1, SLOT_STRIPS):
-                expand(nc.vector.tensor_copy, 0, r, m)
-            load_slot(1, r)
-        for r in range(2):
-            store_tail(0, r)
+        for h in range(HALVES):
+            for m in range(1, ROW_STRIPS):
+                expand(nc.vector.tensor_copy, h, 0, m)
+        nc.sync.dma_start(
+            out=out_0.rearrange("(p h) c j -> p h (c j)", h=HALVES)[:, :, STRIP:], in_=tail_out[0][:]
+        )
 
         mid_words = keep.tile([P, 4 * UNIT_WORDS], U32, name="mid_words", align_bytes=64)
         mid_scales = keep.tile([P, 4 * UNIT_WORDS], U8, name="mid_scales", align_bytes=64)
@@ -228,7 +231,7 @@ def tile_contextualattention_kernel(tc, left, right, mid, sc00, sc01, sc10, sc11
         def first_strip(h, r):
             nc.vector.tensor_copy(
                 out=planes[h][:].rearrange("p (i t) o -> p i t o", t=3)[:, :, 2, :],
-                in_=kept[r][:] if h == 0 else first_strip_shortcuts(r),
+                in_=first_strip_shortcuts(h, r),
             )
             nc.vector.tensor_copy(
                 out=head_out[r][:, h, :].rearrange("p (o j) -> p o j", j=POSITIONS),
@@ -249,11 +252,18 @@ def tile_contextualattention_kernel(tc, left, right, mid, sc00, sc01, sc10, sc11
                         if last_unit(h, i) == u - 1:
                             scores(h, i)
 
-        for m in range(1, SLOT_STRIPS):
-            expand(nc.vector.tensor_copy, 1, 1, m)
-            expand(nc.scalar.copy, 1, 0, m)
-        store_tail(1, 1)
-        store_tail(1, 0)
+        for h in range(HALVES):
+            for m in range(1, ROW_STRIPS):
+                expand(nc.scalar.copy if m == ROW_STRIPS - 1 else nc.vector.tensor_copy, h, 1, m)
+            nc.sync.dma_start(out=dram_rows(out_1, h, B, C), in_=tail_out[1][:, h, :])
+        planes = [
+            keep.tile([P, POSITIONS, B], F32, tag="lc_then_planes%d" % h, name="planes%d" % h, align_bytes=256)
+            for h in range(HALVES)
+        ]
+        head_out = [
+            keep.tile([P, HALVES, STRIP], F32, tag=tag, name="head", align_bytes=256)
+            for tag in ("mid_then_head0", "tail0_then_head1")
+        ]
         for h in range(HALVES):
             for i in range(2):
                 exponentials(h, i)

@@ -20,7 +20,7 @@ STRIP = B * POSITIONS
 ROW_STRIPS = C * POSITIONS // STRIP
 SHORTCUT_STRIPS = 2 * HALVES * ROW_STRIPS
 ZERO_STRIPS = SHORTCUT_STRIPS + 1
-VECTOR_ZERO_STRIPS = 12
+VECTOR_ZERO_STRIPS = 9
 PACK = 4
 K_PASS = P * PACK
 PASSES = C // K_PASS
@@ -82,7 +82,8 @@ def tile_contextualattention_kernel(tc, left, right, mid, sc00, sc01, sc10, sc11
         nc.vector.memset(warm_in[:], 0.0)
         nc.scalar.activation(out=warm_out[:], in_=warm_in[:], func=ACT.Exp)
         nc.vector.memset(padded[:, : VECTOR_ZERO_STRIPS * STRIP].bitcast(F32), 0.0)
-        nc.gpsimd.memset(padded[:, VECTOR_ZERO_STRIPS * STRIP : ZERO_STRIPS * STRIP].bitcast(F32), 0.0)
+        scalar_zeros = padded[:, VECTOR_ZERO_STRIPS * STRIP : ZERO_STRIPS * STRIP].bitcast(F32)
+        nc.scalar.copy(out=scalar_zeros, in_=warm_in[:].to_broadcast([P, (ZERO_STRIPS - VECTOR_ZERO_STRIPS) * STRIP // 2]))
 
         def expand(copy, h, r, m):
             n = (r * HALVES + h) * ROW_STRIPS + m
@@ -229,11 +230,12 @@ def tile_contextualattention_kernel(tc, left, right, mid, sc00, sc01, sc10, sc11
                     )
 
         def first_strip(h, r):
-            nc.vector.tensor_copy(
+            copy = nc.vector.tensor_copy if h == 0 else nc.scalar.copy
+            copy(
                 out=planes[h][:].rearrange("p (i t) o -> p i t o", t=3)[:, :, 2, :],
                 in_=first_strip_shortcuts(h, r),
             )
-            nc.vector.tensor_copy(
+            copy(
                 out=head_out[r][:, h, :].rearrange("p (o j) -> p o j", j=POSITIONS),
                 in_=planes[h][:].rearrange("p j o -> p o j"),
             )
@@ -269,8 +271,7 @@ def tile_contextualattention_kernel(tc, left, right, mid, sc00, sc01, sc10, sc11
                 exponentials(h, i)
         for h in range(HALVES):
             normalise(h)
-            first_strip(h, 0)
-        store_heads(0)
-        for h in range(HALVES):
-            first_strip(h, 1)
-        store_heads(1)
+        for r in range(2):
+            for h in range(HALVES):
+                first_strip(h, r)
+            store_heads(r)

@@ -71,10 +71,17 @@ def tile_contextualattention_kernel(tc, left, right, mid, sc00, sc01, sc10, sc11
                 out=padded[:, first * STRIP : (first + HALVES * ROW_STRIPS) * STRIP], in_=both_rows(shortcuts[r])
             )
 
-        load_shortcuts(0)
+        def load_shortcut_row(h, r):
+            first = ZERO_STRIPS + (r * HALVES + h) * ROW_STRIPS
+            nc.sync.dma_start(
+                out=padded[:, first * STRIP : (first + ROW_STRIPS) * STRIP], in_=dram_rows(shortcuts[r], h, 0, C)
+            )
+
         nc.sync.dma_start(out=mid_sb[:], in_=both_rows(mid))
         nc.sync.dma_start(out=lc_sb[0][:], in_=both_rows(left))
+        load_shortcut_row(0, 0)
         nc.sync.dma_start(out=lc_sb[1][:], in_=both_rows(right))
+        load_shortcut_row(1, 0)
         load_shortcuts(1)
 
         warm_in = keep.tile([P, 1], F32, name="warm_in")
@@ -103,12 +110,10 @@ def tile_contextualattention_kernel(tc, left, right, mid, sc00, sc01, sc10, sc11
                 out=outs[r].rearrange("(p h) c j -> p h (c j)", h=HALVES)[:, :, :STRIP], in_=head_out[r][:]
             )
 
-        for h in range(HALVES):
+        def tail(h, r):
             for m in range(1, ROW_STRIPS):
-                expand(nc.vector.tensor_copy, h, 0, m)
-        nc.sync.dma_start(
-            out=out_0.rearrange("(p h) c j -> p h (c j)", h=HALVES)[:, :, STRIP:], in_=tail_out[0][:]
-        )
+                expand(nc.scalar.copy if m == ROW_STRIPS - 1 else nc.vector.tensor_copy, h, r, m)
+            nc.sync.dma_start(out=dram_rows(outs[r], h, B, C), in_=tail_out[r][:, h, :])
 
         mid_words = keep.tile([P, 4 * UNIT_WORDS], U32, name="mid_words", align_bytes=64)
         mid_scales = keep.tile([P, 4 * UNIT_WORDS], U8, name="mid_scales", align_bytes=64)
@@ -229,8 +234,7 @@ def tile_contextualattention_kernel(tc, left, right, mid, sc00, sc01, sc10, sc11
                         op0=ALU.mult,
                     )
 
-        def first_strip(h, r):
-            copy = nc.vector.tensor_copy if h == 0 else nc.scalar.copy
+        def first_strip(copy, h, r):
             copy(
                 out=planes[h][:].rearrange("p (i t) o -> p i t o", t=3)[:, :, 2, :],
                 in_=first_strip_shortcuts(h, r),
@@ -240,6 +244,7 @@ def tile_contextualattention_kernel(tc, left, right, mid, sc00, sc01, sc10, sc11
                 in_=planes[h][:].rearrange("p j o -> p o j"),
             )
 
+        tails_after = {3: 0, 5: 1}
         for u in range(AHEAD):
             transposes(u)
         for u in range(len(units) + 1):
@@ -249,15 +254,13 @@ def tile_contextualattention_kernel(tc, left, right, mid, sc00, sc01, sc10, sc11
                 transposes(u + AHEAD)
             if u >= 1:
                 quantise(u - 1)
-                for h in range(HALVES):
-                    for i in range(2):
+                for i in range(2):
+                    for h in range(HALVES):
                         if last_unit(h, i) == u - 1:
                             scores(h, i)
+            if u in tails_after:
+                tail(tails_after[u], 0)
 
-        for h in range(HALVES):
-            for m in range(1, ROW_STRIPS):
-                expand(nc.scalar.copy if m == ROW_STRIPS - 1 else nc.vector.tensor_copy, h, 1, m)
-            nc.sync.dma_start(out=dram_rows(out_1, h, B, C), in_=tail_out[1][:, h, :])
         planes = [
             keep.tile([P, POSITIONS, B], F32, tag="lc_then_planes%d" % h, name="planes%d" % h, align_bytes=256)
             for h in range(HALVES)
@@ -266,12 +269,15 @@ def tile_contextualattention_kernel(tc, left, right, mid, sc00, sc01, sc10, sc11
             keep.tile([P, HALVES, STRIP], F32, tag=tag, name="head", align_bytes=256)
             for tag in ("mid_then_head0", "tail0_then_head1")
         ]
-        for h in range(HALVES):
-            for i in range(2):
+        for i in range(2):
+            for h in range(HALVES):
                 exponentials(h, i)
         for h in range(HALVES):
+            tail(h, 1)
+        for h in reversed(range(HALVES)):
             normalise(h)
-        for r in range(2):
-            for h in range(HALVES):
-                first_strip(h, r)
-            store_heads(r)
+            first_strip(nc.vector.tensor_copy, h, 0)
+        store_heads(0)
+        first_strip(nc.vector.tensor_copy, 0, 1)
+        first_strip(nc.scalar.copy, 1, 1)
+        store_heads(1)

from contextlib import ExitStack

import concourse.mybir as mybir
from concourse.masks import make_identity

F32 = mybir.dt.float32
BF16 = mybir.dt.bfloat16
U32 = mybir.dt.uint32
U8 = mybir.dt.uint8
FP8X4 = mybir.dt.float8_e4m3fn_x4
ALU = mybir.AluOpType
ACT = mybir.ActivationFunctionType

P = 128
B = 256
C = 1024
HALVES = B // P
POSITIONS = 6
STRIP = B * POSITIONS
ROW_STRIPS = C * POSITIONS // STRIP
SHORTCUT_STRIPS = 2 * HALVES * ROW_STRIPS
ZERO_STRIPS = SHORTCUT_STRIPS + 1
VECTOR_ZERO_STRIPS = 9
PACK = 4
K_PASS = P * PACK
PASSES = C // K_PASS
UNIT_WORDS = 512
SOFTMAX_SCALE = 10.0
AHEAD = 2

FLOPS = 2 * 2 * (2 * B) * B * (2 * C)
BYTES = 2 * (B * C * 2 * 2) + B * C * 4 * 2 + 2 * (B * C * 2 * 2) + 2 * (B * C * POSITIONS * 4)


def tile_contextualattention_kernel(tc, left, right, mid, sc00, sc01, sc10, sc11, out_0, out_1):
    nc = tc.nc
    outs = (out_0, out_1)
    shortcuts = (sc00, sc10)
    with ExitStack() as ctx:
        keep = ctx.enter_context(tc.tile_pool(name="keep", bufs=1))
        stage = ctx.enter_context(tc.tile_pool(name="stage", bufs=3))
        psum_t = ctx.enter_context(tc.psum_pool(name="psum_t", bufs=4))
        psum_s = ctx.enter_context(tc.psum_pool(name="psum_s", bufs=4))

        ident = keep.tile([P, P], F32, name="ident")
        make_identity(nc, ident[:])

        ctx.enter_context(tc.manual_schedule())

        mid_sb = keep.tile([P, HALVES * C * 4], BF16, tag="mid_then_head0", name="mid_sb", align_bytes=256)
        lc_sb = [
            keep.tile([P, HALVES * C * 2], BF16, tag="lc_then_planes%d" % i, name="lc%d" % i, align_bytes=256)
            for i in range(2)
        ]
        padded = keep.tile([P, (ZERO_STRIPS + SHORTCUT_STRIPS) * STRIP], BF16, name="padded", align_bytes=256)
        strips = padded[:].rearrange("p (n x) -> p n x", x=STRIP)
        tail_out = [
            keep.tile([P, HALVES, (ROW_STRIPS - 1) * STRIP], F32, tag=tag, name="tail", align_bytes=256)
            for tag in ("tail0_then_head1", "tail1")
        ]

        def dram_rows(ap, h, first_channel, end_channel):
            return ap.rearrange("(p h) c j -> p h c j", h=HALVES)[:, h, first_channel:end_channel, :].rearrange("p c j -> p (c j)")

        def both_rows(ap):
            return ap.rearrange("(p h) c j -> p (h c j)", h=HALVES)

        def load_shortcuts(r):
            first = ZERO_STRIPS + r * HALVES * ROW_STRIPS
            nc.sync.dma_start(
                out=padded[:, first * STRIP : (first + HALVES * ROW_STRIPS) * STRIP], in_=both_rows(shortcuts[r])
            )

        def load_shortcut_row(h, r):
            first = ZERO_STRIPS + (r * HALVES + h) * ROW_STRIPS
            nc.sync.dma_start(
                out=padded[:, first * STRIP : (first + ROW_STRIPS) * STRIP], in_=dram_rows(shortcuts[r], h, 0, C)
            )

        nc.sync.dma_start(out=mid_sb[:], in_=both_rows(mid))
        nc.sync.dma_start(out=lc_sb[0][:], in_=both_rows(left))
        load_shortcut_row(0, 0)
        nc.sync.dma_start(out=lc_sb[1][:], in_=both_rows(right))
        load_shortcut_row(1, 0)
        load_shortcuts(1)

        warm_in = keep.tile([P, 1], F32, name="warm_in")
        warm_out = keep.tile([P, 1], F32, name="warm_out")
        nc.vector.memset(warm_in[:], 0.0)
        nc.scalar.activation(out=warm_out[:], in_=warm_in[:], func=ACT.Exp)
        nc.vector.memset(padded[:, : VECTOR_ZERO_STRIPS * STRIP].bitcast(F32), 0.0)
        scalar_zeros = padded[:, VECTOR_ZERO_STRIPS * STRIP : ZERO_STRIPS * STRIP].bitcast(F32)
        nc.scalar.copy(out=scalar_zeros, in_=warm_in[:].to_broadcast([P, (ZERO_STRIPS - VECTOR_ZERO_STRIPS) * STRIP // 2]))

        def expand(copy, h, r, m):
            n = (r * HALVES + h) * ROW_STRIPS + m
            last = ZERO_STRIPS + n
            step = n + 1
            src = strips[:, last - 2 * step : last + 1 : step, :]
            src = src.rearrange("p t (c j) -> p c j t", j=POSITIONS)[:, :, 0:2, :]
            dst = tail_out[r][:, h, (m - 1) * STRIP : m * STRIP].rearrange("p (c i t) -> p c i t", i=2, t=3)
            copy(out=dst, in_=src)

        def first_strip_shortcuts(h, r):
            row = strips[:, ZERO_STRIPS + (r * HALVES + h) * ROW_STRIPS, :]
            return row.rearrange("p (o j) -> p j o", j=POSITIONS)[:, 0:2, :]

        def store_heads(r):
            nc.sync.dma_start(
                out=outs[r].rearrange("(p h) c j -> p h (c j)", h=HALVES)[:, :, :STRIP], in_=head_out[r][:]
            )

        def tail(h, r):
            for m in range(1, ROW_STRIPS):
                expand(nc.scalar.copy if m == ROW_STRIPS - 1 else nc.vector.tensor_copy, h, r, m)
            nc.sync.dma_start(out=dram_rows(outs[r], h, B, C), in_=tail_out[r][:, h, :])

        mid_words = keep.tile([P, 4 * UNIT_WORDS], U32, name="mid_words", align_bytes=64)
        mid_scales = keep.tile([P, 4 * UNIT_WORDS], U8, name="mid_scales", align_bytes=64)
        lc_words = keep.tile([P, 4 * UNIT_WORDS], U32, name="lc_words", align_bytes=64)
        lc_scales = keep.tile([P, 4 * UNIT_WORDS], U8, name="lc_scales", align_bytes=64)

        units = [(kind, x, y) for kind in ("mid", "lc") for x in range(2) for y in range(2)]
        bank_tiles = {}
        column_tiles = {}

        def transposes(u):
            kind, a, b = units[u]
            for half in range(2):
                bank = psum_t.tile([P, PACK * P], F32, tag="bank", name="bank")
                bank_tiles[(u, half)] = bank
                for v in range(PACK):
                    if kind == "mid":
                        c0 = a * C + K_PASS * half + P * v
                        src = mid_sb[:].bitcast(F32).rearrange("b (c i) -> b c i", i=2)[:, c0 : c0 + P, b]
                    else:
                        c0 = half * C + K_PASS * b + P * v
                        src = lc_sb[a][:].bitcast(F32)[:, c0 : c0 + P]
                    nc.tensor.transpose(bank[:, v * P : (v + 1) * P], src, ident[:])

        def copy_out(u):
            kind, a, b = units[u]
            columns = stage.tile([P, 2, 2, P, PACK], BF16, tag="columns", name="columns", align_bytes=64)
            column_tiles[u] = columns
            for half in range(2):
                dst = columns[:, half] if kind == "mid" else columns[:, :, half]
                src = bank_tiles[(u, half)][:].bitcast(BF16).rearrange("p (v w e) -> p e w v", v=PACK, w=P, e=2)
                if half == 1 and (a, b) != (1, 1):
                    nc.vector.tensor_copy(out=dst, in_=src)
                else:
                    nc.scalar.copy(out=dst, in_=src)

        def quantise(u):
            kind, a, b = units[u]
            words, scales = (mid_words, mid_scales) if kind == "mid" else (lc_words, lc_scales)
            cols = slice((2 * a + b) * UNIT_WORDS, (2 * a + b + 1) * UNIT_WORDS)
            nc.vector.quantize_mx(
                out=words[:, cols].bitcast(FP8X4),
                scales=scales[:, cols],
                in_=column_tiles[u][:].rearrange("p x y w v -> p (x y w v)"),
            )

        row_maxima = keep.tile([P, 8], F32, name="row_maxima")
        biases = keep.tile([P, 8], F32, name="biases")
        sums = keep.tile([P, 8], F32, name="sums")
        inverse_sums = keep.tile([P, 8], F32, name="inverse_sums")
        score_tiles = {}

        def mid_cols(h, i, g, e):
            lo = (((h * 2 + i) * 2 + g) * 2 + e) * P
            return slice(lo, lo + P)

        def lc_cols(i, g, e):
            lo = ((i * 2 + g) * 2 + e) * B
            return slice(lo, lo + B)

        def last_unit(h, i):
            return max(units.index(("mid", h, i)), units.index(("lc", i, PASSES - 1)))

        def scores(h, i):
            bank = psum_s.tile([P, 2 * B], F32, tag="scores", name="scores")
            score_tiles[(h, i)] = bank
            taps = (
                [(g, 0, 1) for g in range(PASSES)],
                [(g, e, e) for g in range(PASSES) for e in range(2)],
            )
            for t in range(2):
                for n, (g, e_mid, e_lc) in enumerate(taps[t]):
                    nc.tensor.matmul_mx(
                        out=bank[:, t * B : (t + 1) * B],
                        lhsT=mid_words[:, mid_cols(h, i, g, e_mid)].bitcast(FP8X4),
                        lhsT_scale=mid_scales[:, mid_cols(h, i, g, e_mid)],
                        rhs=lc_words[:, lc_cols(i, g, e_lc)].bitcast(FP8X4),
                        rhs_scale=lc_scales[:, lc_cols(i, g, e_lc)],
                        start=(n == 0),
                        stop=(n == len(taps[t]) - 1),
                    )

        def exponentials(h, i):
            col = (h * 2 + i) * 2
            nc.vector.tensor_reduce(
                out=row_maxima[:, col : col + 2],
                in_=score_tiles[(h, i)][:].rearrange("p (t o) -> p t o", t=2),
                axis=mybir.AxisListType.X,
                op=ALU.max,
            )
            nc.vector.tensor_scalar(
                out=biases[:, col : col + 2],
                in0=row_maxima[:, col : col + 2],
                scalar1=-SOFTMAX_SCALE,
                scalar2=None,
                op0=ALU.mult,
            )
            for t in range(2):
                nc.scalar.activation(
                    out=planes[h][:, 3 * i + t, :].rearrange("p (w ho) -> p w ho", ho=HALVES),
                    in_=score_tiles[(h, i)][:, t * B : (t + 1) * B].rearrange("p (ho w) -> p w ho", ho=HALVES),
                    func=ACT.Exp,
                    bias=biases[:, col + t : col + t + 1],
                    scale=SOFTMAX_SCALE,
                    accum_out=sums[:, col + t : col + t + 1],
                )

        def normalise(h):
            nc.vector.reciprocal(out=inverse_sums[:, 4 * h : 4 * h + 4], in_=sums[:, 4 * h : 4 * h + 4])
            for i in range(2):
                for t in range(2):
                    col = (h * 2 + i) * 2 + t
                    nc.vector.tensor_scalar(
                        out=planes[h][:, 3 * i + t, :],
                        in0=planes[h][:, 3 * i + t, :],
                        scalar1=inverse_sums[:, col : col + 1],
                        scalar2=None,
                        op0=ALU.mult,
                    )

        def first_strip(copy, h, r):
            copy(
                out=planes[h][:].rearrange("p (i t) o -> p i t o", t=3)[:, :, 2, :],
                in_=first_strip_shortcuts(h, r),
            )
            copy(
                out=head_out[r][:, h, :].rearrange("p (o j) -> p o j", j=POSITIONS),
                in_=planes[h][:].rearrange("p j o -> p o j"),
            )

        tails_after = {3: 0, 5: 1}
        for u in range(AHEAD):
            transposes(u)
        for u in range(len(units) + 1):
            if u < len(units):
                copy_out(u)
            if u + AHEAD < len(units):
                transposes(u + AHEAD)
            if u >= 1:
                quantise(u - 1)
                for i in range(2):
                    for h in range(HALVES):
                        if last_unit(h, i) == u - 1:
                            scores(h, i)
            if u in tails_after:
                tail(tails_after[u], 0)

        planes = [
            keep.tile([P, POSITIONS, B], F32, tag="lc_then_planes%d" % h, name="planes%d" % h, align_bytes=256)
            for h in range(HALVES)
        ]
        head_out = [
            keep.tile([P, HALVES, STRIP], F32, tag=tag, name="head", align_bytes=256)
            for tag in ("mid_then_head0", "tail0_then_head1")
        ]
        for i in range(2):
            for h in range(HALVES):
                exponentials(h, i)
        for h in range(HALVES):
            tail(h, 1)
        for h in reversed(range(HALVES)):
            normalise(h)
            first_strip(nc.vector.tensor_copy, h, 0)
        store_heads(0)
        first_strip(nc.vector.tensor_copy, 0, 1)
        first_strip(nc.scalar.copy, 1, 1)
        store_heads(1)
